import numpy as np
import ml_dtypes


def mxq(x, axis, fmt="e4m3"):
    dtype, down = {"e4m3": (ml_dtypes.float8_e4m3fn, 7), "e5m2": (ml_dtypes.float8_e5m2, 14)}[fmt]
    v = np.moveaxis(np.asarray(x, np.float32).astype(ml_dtypes.bfloat16).astype(np.float64), axis, -1)
    blocks = v.reshape(v.shape[:-1] + (-1, 32))
    amax = np.abs(blocks).max(-1, keepdims=True)
    byte = np.maximum(np.where(amax > 0, np.frexp(amax)[1] - 1 + 127, 0) - down, 1)
    scale = np.exp2(byte - 127.0)
    codes = (blocks / scale).astype(np.float32).astype(dtype).astype(np.float64)
    return np.moveaxis((codes * scale).reshape(v.shape), -1, axis)


WIDE = False


def mx_kscale(k):
    if not WIDE:
        return np.ones(k)
    levels = np.array([10, -10, 5, -5, 0])
    if k % 512:
        return np.exp2(np.random.permutation(np.resize(levels, k // 32))).repeat(32)
    a = np.empty((k // 512, 16))
    for p in range(k // 512):
        a[p, :8] = np.random.permutation(np.resize(levels, 8))
        for g in range(8):
            far = levels[np.abs(levels - a[p, g]) >= 10]
            a[p, g + 8] = far[np.random.randint(len(far))]
    return np.exp2(a.ravel()).repeat(32)


BF16 = ml_dtypes.bfloat16


def bf(x):
    return np.asarray(x, np.float32).astype(BF16)


def f64(x):
    return np.asarray(x).astype(np.float64)


B, S, D, H, QL, KVL, NOPE, ROPE, VD = 2, 256, 2048, 16, 1536, 512, 128, 128, 128
HALF = ROPE // 2
ROPE_BASE = 10000.0
EPS = 1e-6


def rmsnorm(x, w):
    return x * (1.0 / np.sqrt(np.mean(x * x, axis=-1, keepdims=True) + EPS)) * w


def rope_tables():
    inv_freq = 1.0 / ROPE_BASE ** (np.arange(HALF) / HALF)
    ang = np.arange(S)[:, None] * inv_freq
    return np.cos(ang), np.sin(ang)


def rope(x, cos, sin):
    x1, x2 = x[..., :HALF], x[..., HALF:]
    return np.concatenate([x1 * cos - x2 * sin, x1 * sin + x2 * cos], axis=-1)


def setup_inputs():
    s, t = mx_kscale(D), mx_kscale(KVL)
    return {
        "hidden_states": bf(np.random.standard_normal((B, S, D)) * s),
        "w_kv_a": bf(np.random.standard_normal((D, KVL + ROPE)) / np.sqrt(D) / s[:, None]),
        "kv_a_ln_w": bf((1.0 + 0.1 * np.random.standard_normal(KVL)) * t),
        "w_kv_b": bf(np.random.standard_normal((KVL, H * (NOPE + VD))) / np.sqrt(KVL) / t[:, None]),
    }


def reference(hidden_states, w_kv_a, kv_a_ln_w, w_kv_b):
    fused = mxq(f64(hidden_states), 2, "e4m3") @ mxq(f64(w_kv_a), 0, "e4m3")
    kv_c, k_pe = fused[..., :KVL], fused[..., KVL:]
    kv_n = rmsnorm(kv_c, f64(kv_a_ln_w))
    kv = (mxq(kv_n, 2, "e4m3") @ mxq(f64(w_kv_b), 0, "e4m3")).reshape(B, S, H, NOPE + VD)
    k_nope, v = kv[..., :NOPE], kv[..., NOPE:]
    cos, sin = rope_tables()
    k_pe = rope(k_pe, cos[None], sin[None])
    k = np.concatenate([k_nope, np.broadcast_to(k_pe[:, :, None, :], (B, S, H, ROPE))], axis=-1)
    return k, v

@@ -1,0 +1,381 @@
+import math
+from contextlib import ExitStack
+
+import concourse.mybir as mybir
+from concourse.masks import make_identity
+
+F32 = mybir.dt.float32
+BF16 = mybir.dt.bfloat16
+I32 = mybir.dt.int32
+U32 = mybir.dt.uint32
+U8 = mybir.dt.uint8
+FP8X4 = mybir.dt.float8_e4m3fn_x4
+ALU = mybir.AluOpType
+ACT = mybir.ActivationFunctionType
+
+P = 128
+PACK = 4
+K_PASS = P * PACK
+BANK = 512
+
+TOKENS = 512
+TOKEN_TILES = TOKENS // P
+D_MODEL = 2048
+PASSES_A = D_MODEL // K_PASS
+LATENT = 512
+ROPE = 128
+HALF = ROPE // 2
+HALF_LOG2 = 6
+assert 2**HALF_LOG2 == HALF
+FUSED = LATENT + ROPE
+HEADS = 16
+NOPE = 128
+V_DIM = 128
+KINDS = 2
+KIND_K_NOPE = 0
+KIND_V = 1
+ROPE_BASE = 10000.0
+EPS = 1e-6
+
+PIECE_HEADS = BANK // NOPE
+PIECE_COLS = PIECE_HEADS * (NOPE + V_DIM)
+PIECES = HEADS // PIECE_HEADS
+
+RUN = 4
+A_SPLIT = FUSED // 2
+
+ROUND_MAGIC = 1.5 * 2.0**23
+
+FLOPS = 2 * TOKENS * D_MODEL * FUSED + 2 * TOKENS * LATENT * HEADS * (NOPE + V_DIM)
+
+
+def tile_mla_pb_kernel(tc, hidden_states, w_kv_a, kv_a_ln_w, w_kv_b, out_0, out_1):
+    nc = tc.nc
+    hidden = hidden_states.flatten_outer_dims()
+    k_out = out_0.rearrange("b s h c -> (b s) h c")
+    v_out = out_1.rearrange("b s h c -> (b s) h c")
+
+    with ExitStack() as ctx:
+        ctx.enter_context(tc.manual_schedule())
+        consts = ctx.enter_context(tc.tile_pool(name="consts", bufs=1))
+        resident = ctx.enter_context(tc.tile_pool(name="resident", bufs=1))
+        stage = ctx.enter_context(tc.tile_pool(name="stage", bufs=2))
+        pieces = ctx.enter_context(tc.tile_pool(name="pieces", bufs=8))
+        psum = ctx.enter_context(tc.psum_pool(name="psum", bufs=4))
+
+        gain_row = consts.tile([P, LATENT], BF16)
+        nc.vector.memset(gain_row[:], 0.0)
+        x_rows = []
+        for tt in range(TOKEN_TILES):
+            rows = resident.tile([P, D_MODEL], BF16, name="x_rows%d" % tt)
+            nc.sync.dma_start(out=rows[:], in_=hidden[tt * P : (tt + 1) * P, :])
+            x_rows.append(rows)
+            if tt == 0:
+                nc.sync.dma_start(out=gain_row[0:1, :], in_=kv_a_ln_w.unsqueeze(0))
+        raw_a = []
+        for g in range(PASSES_A):
+            raw = resident.tile([P, PACK, FUSED], BF16, name="raw_a%d" % g)
+            rows = w_kv_a[g * K_PASS : (g + 1) * K_PASS, :]
+            nc.sync.dma_start(
+                out=raw[:], in_=rows.rearrange("(p t) c -> p t c", t=PACK)
+            )
+            raw_a.append(raw)
+        raw_b = []
+        for j in range(PIECES):
+            raw = resident.tile([P, PACK, PIECE_COLS], BF16, name="raw_b%d" % j)
+            cols = w_kv_b[:, j * PIECE_COLS : (j + 1) * PIECE_COLS]
+            nc.sync.dma_start(out=raw[:], in_=cols.rearrange("(p t) n -> p t n", t=PACK))
+            raw_b.append(raw)
+
+        position = consts.tile([P, 2], I32)
+        nc.gpsimd.iota(position[:], pattern=[[P, 2]], base=0, channel_multiplier=1)
+        inv_freq = consts.tile([P, HALF], F32)
+        nc.vector.memset(inv_freq[:, 0:1], 1.0)
+        for level in range(HALF_LOG2):
+            width = 2**level
+            nc.vector.tensor_scalar(
+                out=inv_freq[:, width : 2 * width], in0=inv_freq[:, 0:width],
+                scalar1=ROPE_BASE ** (-width / HALF), scalar2=None, op0=ALU.mult,
+            )
+        position_turns = consts.tile([P, 2], F32)
+        nc.vector.tensor_scalar(
+            out=position_turns[:], in0=position[:], scalar1=1.0 / (2.0 * math.pi), scalar2=None,
+            op0=ALU.mult,
+        )
+        phases = (0.5, 0.25, 0.0)
+        turns = consts.tile([P, 2, len(phases), HALF], F32)
+        for a in range(2):
+            for i, phase in enumerate(phases):
+                nc.vector.tensor_scalar(
+                    out=turns[:, a, i, :], in0=inv_freq[:], scalar1=position_turns[:, a : a + 1],
+                    scalar2=phase, op0=ALU.mult, op1=ALU.add,
+                )
+        whole_turns = consts.tile([P, 2, len(phases), HALF], F32)
+        nc.vector.tensor_scalar(
+            out=whole_turns[:], in0=turns[:], scalar1=ROUND_MAGIC, scalar2=ROUND_MAGIC,
+            op0=ALU.add, op1=ALU.subtract,
+        )
+        part_turns = consts.tile([P, 2, len(phases), HALF], F32)
+        nc.vector.tensor_tensor(out=part_turns[:], in0=turns[:], in1=whole_turns[:], op=ALU.subtract)
+        table = consts.tile([P, 2, len(phases), HALF], F32)
+        nc.scalar.activation(out=table[:], in_=part_turns[:], func=ACT.Sin, scale=2.0 * math.pi)
+
+        square_sum = consts.tile([P, TOKEN_TILES], F32)
+        rms = consts.tile([P, TOKEN_TILES], F32)
+        inv_rms = consts.tile([P, TOKEN_TILES], F32)
+        nc.scalar.activation(out=rms[:, 0:1], in_=inv_freq[:, 0:1], func=ACT.Sqrt)
+
+        ident_f32 = consts.tile([P, P], F32)
+        make_identity(nc, ident_f32[:])
+        ones = consts.tile([P, P], BF16)
+        nc.vector.memset(ones[:], 1.0)
+        gain_ps = psum.tile([P, LATENT], F32, tag="right")
+        nc.tensor.matmul(out=gain_ps[:], lhsT=ones[:], rhs=gain_row[:], start=True, stop=True)
+        gain = consts.tile([P, LATENT], BF16)
+        nc.vector.tensor_copy(out=gain[:], in_=gain_ps[:])
+
+        x_codes = resident.tile([P, TOKEN_TILES, PASSES_A * P], U32, align_bytes=64)
+        x_scales = resident.tile([P, TOKEN_TILES, PASSES_A * P], U8, align_bytes=64)
+        grouped_x = []
+
+        def flip_hidden(tt):
+            words = x_rows[tt][:].bitcast(F32)
+            grouped = stage.tile([P, PASSES_A * P * PACK], BF16, align_bytes=64, tag="grouped_x")
+            grouped_words = grouped[:].bitcast(F32).rearrange("p (g k u) -> p g k u", g=PASSES_A, u=2)
+            for ring, copy, first_pass in (
+                ("left", nc.scalar.copy, 0),
+                ("right", nc.vector.tensor_copy, 2),
+            ):
+                flipped = psum.tile([P, 2, 2, P], F32, tag=ring)
+                for gg in range(2):
+                    for u in range(2):
+                        first = (first_pass + gg) * (K_PASS // 2)
+                        nc.tensor.transpose(
+                            flipped[:, gg, u, :],
+                            words[:, first + u : first + K_PASS // 2 : 2],
+                            ident_f32[:],
+                        )
+                copy(
+                    out=grouped_words[:, first_pass : first_pass + 2, :, :],
+                    in_=flipped[:].rearrange("p g u k -> p g k u"),
+                )
+            grouped_x.append(grouped)
+
+        flip_hidden(0)
+        for tt in range(TOKEN_TILES):
+            if tt + 1 < TOKEN_TILES:
+                flip_hidden(tt + 1)
+            nc.vector.quantize_mx(
+                out=x_codes[:, tt, :].bitcast(FP8X4), scales=x_scales[:, tt, :], in_=grouped_x[tt][:]
+            )
+
+        a_codes = resident.tile([P, PASSES_A, FUSED], U32, align_bytes=64)
+        a_scales = resident.tile([P, PASSES_A, FUSED], U8, align_bytes=64)
+        grouped_a = []
+        latent_ps = []
+        rope_ps = []
+
+        def regroup_a(g):
+            grouped = stage.tile(
+                [P, FUSED, PACK], BF16, align_bytes=64, tag="grouped_a", bufs=PASSES_A
+            )
+            for copy, cols in (
+                (nc.vector.tensor_copy, slice(0, A_SPLIT)),
+                (nc.scalar.copy, slice(A_SPLIT, FUSED)),
+            ):
+                copy(
+                    out=grouped[:, cols, :].rearrange("p (c i) t -> p c t i", i=RUN),
+                    in_=raw_a[g][:, :, cols].rearrange("p t (c i) -> p c t i", i=RUN),
+                )
+            grouped_a.append(grouped)
+
+        def quantise_a(g):
+            for cols in (slice(0, LATENT), slice(LATENT, FUSED)):
+                nc.vector.quantize_mx(
+                    out=a_codes[:, g, cols].bitcast(FP8X4),
+                    scales=a_scales[:, g, cols],
+                    in_=grouped_a[g][:, cols, :].rearrange("p c t -> p (c t)"),
+                )
+
+        def first_product(g):
+            of_pass = slice(g * P, (g + 1) * P)
+            for tt in range(TOKEN_TILES):
+                if g == 0:
+                    latent_ps.append(psum.tile([P, LATENT], F32, name="latent_ps", tag="left"))
+                    rope_ps.append(psum.tile([P, ROPE], F32, name="rope_ps", tag="right"))
+                for acc, cols in (
+                    (latent_ps[tt], slice(0, LATENT)),
+                    (rope_ps[tt], slice(LATENT, FUSED)),
+                ):
+                    nc.tensor.matmul_mx(
+                        out=acc[:],
+                        lhsT=x_codes[:, tt, of_pass].bitcast(FP8X4),
+                        lhsT_scale=x_scales[:, tt, of_pass],
+                        rhs=a_codes[:, g, cols].bitcast(FP8X4),
+                        rhs_scale=a_scales[:, g, cols],
+                        start=(g == 0),
+                        stop=(g == PASSES_A - 1),
+                    )
+
+        regroup_a(0)
+        for g in range(PASSES_A):
+            if g + 1 < PASSES_A:
+                regroup_a(g + 1)
+            quantise_a(g)
+            first_product(g)
+
+        n_codes = resident.tile([P, TOKEN_TILES, P], U32, align_bytes=64)
+        n_scales = resident.tile([P, TOKEN_TILES, P], U8, align_bytes=64)
+        b_codes = resident.tile([P, PIECES, KINDS, BANK], U32, align_bytes=64)
+        b_scales = resident.tile([P, PIECES, KINDS, BANK], U8, align_bytes=64)
+        kv_n = {}
+        flipped_n = {}
+        grouped_n = {}
+        grouped_b = {}
+        k_pe = {}
+        k_pieces = {}
+
+        def sum_squares(tt):
+            squares = stage.tile([P, LATENT], BF16)
+            nc.scalar.activation(
+                out=squares[:], in_=latent_ps[tt][:], func=ACT.Square,
+                accum_out=square_sum[:, tt : tt + 1],
+            )
+
+        def root_mean_square(tt):
+            nc.scalar.activation(
+                out=rms[:, tt : tt + 1], in_=square_sum[:, tt : tt + 1], func=ACT.Sqrt,
+                bias=EPS, scale=1.0 / LATENT,
+            )
+
+        def invert_rms(tt):
+            nc.vector.reciprocal(out=inv_rms[:, tt : tt + 1], in_=rms[:, tt : tt + 1])
+
+        def normalise(tt):
+            kv_n[tt] = stage.tile([P, LATENT], BF16, name="kv_n", tag="kv_n")
+            nc.vector.scalar_tensor_tensor(
+                out=kv_n[tt][:], in0=latent_ps[tt][:], scalar=inv_rms[:, tt : tt + 1], in1=gain[:],
+                op0=ALU.mult, op1=ALU.mult,
+            )
+
+        def flip_kv_n(tt):
+            words = kv_n[tt][:].bitcast(F32)
+            flipped_n[tt] = psum.tile([P, 2, P], F32, name="flipped_n", tag="right")
+            for u in range(2):
+                nc.tensor.transpose(flipped_n[tt][:, u, :], words[:, u : K_PASS // 2 : 2], ident_f32[:])
+            grouped_n[tt] = stage.tile(
+                [P, P * PACK], BF16, align_bytes=64, name="grouped_n", tag="grouped_n"
+            )
+            nc.scalar.copy(
+                out=grouped_n[tt][:].bitcast(F32).rearrange("p (k u) -> p k u", u=2),
+                in_=flipped_n[tt][:].rearrange("p u k -> p k u"),
+            )
+
+        def quantise_kv_n(tt):
+            nc.vector.quantize_mx(
+                out=n_codes[:, tt, :].bitcast(FP8X4),
+                scales=n_scales[:, tt, :],
+                in_=grouped_n[tt][:],
+            )
+
+        def rotate(tt):
+            x = stage.tile([P, ROPE], F32, name="rope_x", tag="rope_x")
+            nc.scalar.copy(out=x[:], in_=rope_ps[tt][:])
+            a = tt % 2
+            x1 = x[:, 0:HALF].unsqueeze(1).to_broadcast([P, 2, HALF])
+            x2 = x[:, HALF:ROPE].unsqueeze(1).to_broadcast([P, 2, HALF])
+            from_x1 = stage.tile([P, 2, HALF], F32)
+            nc.gpsimd.tensor_tensor(out=from_x1[:], in0=x1, in1=table[:, a, 1:3, :], op=ALU.mult)
+            from_x2 = stage.tile([P, 2, HALF], F32)
+            nc.gpsimd.tensor_tensor(out=from_x2[:], in0=x2, in1=table[:, a, 0:2, :], op=ALU.mult)
+            k_pe[tt] = consts.tile([P, 2, HALF], F32, name="k_pe%d" % tt)
+            nc.gpsimd.tensor_tensor(out=k_pe[tt][:], in0=from_x1[:], in1=from_x2[:], op=ALU.add)
+
+        def spread_k_pe(j, tt):
+            k_pieces[j, tt] = pieces.tile(
+                [P, PIECE_HEADS, NOPE + ROPE], F32, name="k_piece", tag="k_piece"
+            )
+            nc.gpsimd.tensor_scalar(
+                out=k_pieces[j, tt][:, :, NOPE:],
+                in0=k_pe[tt][:].rearrange("p h c -> p (h c)").unsqueeze(1).to_broadcast(
+                    [P, PIECE_HEADS, ROPE]
+                ),
+                scalar1=1.0, scalar2=0.0, op0=ALU.mult, op1=ALU.add,
+            )
+
+        def regroup_b(j, kind):
+            grouped_b[j, kind] = stage.tile(
+                [P, BANK, PACK], BF16, align_bytes=64, name="grouped_b", tag="grouped_b"
+            )
+            by_kind = raw_b[j][:].rearrange(
+                "p t (h s c i) -> p s h c t i", h=PIECE_HEADS, s=KINDS, i=RUN
+            )
+            nc.vector.tensor_copy(
+                out=grouped_b[j, kind][:].rearrange("p (h c i) t -> p h c t i", h=PIECE_HEADS, i=RUN),
+                in_=by_kind[:, kind],
+            )
+
+        def quantise_b(j, kind):
+            nc.vector.quantize_mx(
+                out=b_codes[:, j, kind, :].bitcast(FP8X4),
+                scales=b_scales[:, j, kind, :],
+                in_=grouped_b[j, kind][:].rearrange("p c t -> p (c t)"),
+            )
+
+        def multiply_b(j, tt, kind, ring):
+            kv_ps = psum.tile([P, BANK], F32, name="kv_ps", tag=ring)
+            nc.tensor.matmul_mx(
+                out=kv_ps[:],
+                lhsT=n_codes[:, tt, :].bitcast(FP8X4),
+                lhsT_scale=n_scales[:, tt, :],
+                rhs=b_codes[:, j, kind, :].bitcast(FP8X4),
+                rhs_scale=b_scales[:, j, kind, :],
+                start=True,
+                stop=True,
+            )
+            return kv_ps[:].rearrange("p (h c) -> p h c", h=PIECE_HEADS)
+
+        def second_product(j, tt):
+            if j + 1 < PIECES:
+                if tt % 2 == 0:
+                    regroup_b(j + 1, tt // 2)
+                else:
+                    quantise_b(j + 1, tt // 2)
+            tokens = slice(tt * P, (tt + 1) * P)
+            heads = slice(j * PIECE_HEADS, (j + 1) * PIECE_HEADS)
+            nc.scalar.copy(out=k_pieces[j, tt][:, :, :NOPE], in_=multiply_b(j, tt, KIND_K_NOPE, "left"))
+            nc.sync.dma_start(out=k_out[tokens, heads, :], in_=k_pieces[j, tt][:])
+            v_piece = pieces.tile([P, PIECE_HEADS, V_DIM], F32)
+            copy = nc.vector.tensor_copy if tt % 2 == 1 else nc.scalar.copy
+            copy(out=v_piece[:], in_=multiply_b(j, tt, KIND_V, "right"))
+            nc.sync.dma_start(out=v_out[tokens, heads, :], in_=v_piece[:])
+
+        for kind in range(KINDS):
+            regroup_b(0, kind)
+        for kind in range(KINDS):
+            quantise_b(0, kind)
+
+        def is_tile(tt):
+            return 0 <= tt < TOKEN_TILES
+
+        for step in range(TOKEN_TILES + 4):
+            if is_tile(step - 1):
+                invert_rms(step - 1)
+            if is_tile(step - 3):
+                quantise_kv_n(step - 3)
+            if is_tile(step - 1):
+                normalise(step - 1)
+            if is_tile(step - 4):
+                second_product(0, step - 4)
+            if is_tile(step):
+                sum_squares(step)
+                rotate(step)
+                spread_k_pe(0, step)
+                root_mean_square(step)
+            if is_tile(step - 2):
+                flip_kv_n(step - 2)
+
+        for j in range(1, PIECES):
+            for tt in range(TOKEN_TILES):
+                spread_k_pe(j, tt)
+                second_product(j, tt)

@@ -5,8 +5,8 @@ import concourse.mybir as mybir
 from concourse.masks import make_identity
 
 F32 = mybir.dt.float32
-BF16 = mybir.dt.bfloat16
 I32 = mybir.dt.int32
+BF16 = mybir.dt.bfloat16
 U32 = mybir.dt.uint32
 U8 = mybir.dt.uint8
 FP8X4 = mybir.dt.float8_e4m3fn_x4
@@ -41,7 +41,10 @@ PIECE_HEADS = BANK // NOPE
 PIECE_COLS = PIECE_HEADS * (NOPE + V_DIM)
 PIECES = HEADS // PIECE_HEADS
 
+KEY_TILES = 2
+
 RUN = 4
+B_SPLIT = 96
 A_SPLIT = FUSED // 2
 
 ROUND_MAGIC = 1.5 * 2.0**23
@@ -61,34 +64,52 @@ def tile_mla_pb_kernel(tc, hidden_states, w_kv_a, kv_a_ln_w, w_kv_b, out_0, out_
         resident = ctx.enter_context(tc.tile_pool(name="resident", bufs=1))
         stage = ctx.enter_context(tc.tile_pool(name="stage", bufs=2))
         pieces = ctx.enter_context(tc.tile_pool(name="pieces", bufs=8))
-        psum = ctx.enter_context(tc.psum_pool(name="psum", bufs=4))
+        psum = ctx.enter_context(tc.psum_pool(name="psum", bufs=2))
 
+        x_rows = {}
+        raw_a = {}
+        raw_b = {}
         gain_row = consts.tile([P, LATENT], BF16)
-        nc.vector.memset(gain_row[:], 0.0)
-        x_rows = []
-        for tt in range(TOKEN_TILES):
-            rows = resident.tile([P, D_MODEL], BF16, name="x_rows%d" % tt)
-            nc.sync.dma_start(out=rows[:], in_=hidden[tt * P : (tt + 1) * P, :])
-            x_rows.append(rows)
-            if tt == 0:
-                nc.sync.dma_start(out=gain_row[0:1, :], in_=kv_a_ln_w.unsqueeze(0))
-        raw_a = []
-        for g in range(PASSES_A):
-            raw = resident.tile([P, PACK, FUSED], BF16, name="raw_a%d" % g)
+
+        def load_x(tt):
+            x_rows[tt] = resident.tile([P, D_MODEL], BF16, name="x_rows%d" % tt)
+            nc.sync.dma_start(out=x_rows[tt][:], in_=hidden[tt * P : (tt + 1) * P, :])
+
+        def load_gain():
+            nc.sync.dma_start(out=gain_row[0:1, :], in_=kv_a_ln_w.unsqueeze(0))
+
+        def load_a(g):
+            raw_a[g] = resident.tile([P, PACK, FUSED], BF16, name="raw_a%d" % g)
             rows = w_kv_a[g * K_PASS : (g + 1) * K_PASS, :]
-            nc.sync.dma_start(
-                out=raw[:], in_=rows.rearrange("(p t) c -> p t c", t=PACK)
-            )
-            raw_a.append(raw)
-        raw_b = []
-        for j in range(PIECES):
-            raw = resident.tile([P, PACK, PIECE_COLS], BF16, name="raw_b%d" % j)
+            nc.sync.dma_start(out=raw_a[g][:], in_=rows.rearrange("(p t) c -> p t c", t=PACK))
+
+        def load_b(j):
+            raw_b[j] = resident.tile([P, PACK, PIECE_COLS], BF16, name="raw_b%d" % j)
             cols = w_kv_b[:, j * PIECE_COLS : (j + 1) * PIECE_COLS]
-            nc.sync.dma_start(out=raw[:], in_=cols.rearrange("(p t) n -> p t n", t=PACK))
-            raw_b.append(raw)
+            nc.sync.dma_start(out=raw_b[j][:], in_=cols.rearrange("(p t) n -> p t n", t=PACK))
 
         position = consts.tile([P, 2], I32)
         nc.gpsimd.iota(position[:], pattern=[[P, 2]], base=0, channel_multiplier=1)
+        ident_f32 = consts.tile([P, P], F32)
+        make_identity(nc, ident_f32[:])
+        nc.gpsimd.memset(gain_row[:], 0.0)
+        ones = consts.tile([P, P], BF16)
+        nc.gpsimd.memset(ones[:], 1.0)
+        load_x(0)
+        load_gain()
+        for g in range(PASSES_A):
+            load_a(g)
+        load_x(1)
+        load_x(2)
+        load_b(0)
+        load_x(3)
+        for j in range(1, PIECES):
+            load_b(j)
+
+        warm = consts.tile([P, 1], F32)
+        nc.vector.memset(warm[:], 0.0)
+        warm_out = consts.tile([P, 1], F32)
+        nc.scalar.activation(out=warm_out[:], in_=warm[:], func=ACT.Sin)
         inv_freq = consts.tile([P, HALF], F32)
         nc.vector.memset(inv_freq[:, 0:1], 1.0)
         for level in range(HALF_LOG2):
@@ -121,73 +142,63 @@ def tile_mla_pb_kernel(tc, hidden_states, w_kv_a, kv_a_ln_w, w_kv_b, out_0, out_
         nc.scalar.activation(out=table[:], in_=part_turns[:], func=ACT.Sin, scale=2.0 * math.pi)
 
         square_sum = consts.tile([P, TOKEN_TILES], F32)
-        rms = consts.tile([P, TOKEN_TILES], F32)
         inv_rms = consts.tile([P, TOKEN_TILES], F32)
-        nc.scalar.activation(out=rms[:, 0:1], in_=inv_freq[:, 0:1], func=ACT.Sqrt)
-
-        ident_f32 = consts.tile([P, P], F32)
-        make_identity(nc, ident_f32[:])
-        ones = consts.tile([P, P], BF16)
-        nc.vector.memset(ones[:], 1.0)
-        gain_ps = psum.tile([P, LATENT], F32, tag="right")
-        nc.tensor.matmul(out=gain_ps[:], lhsT=ones[:], rhs=gain_row[:], start=True, stop=True)
-        gain = consts.tile([P, LATENT], BF16)
-        nc.vector.tensor_copy(out=gain[:], in_=gain_ps[:])
+        nc.scalar.activation(out=inv_rms[:, 0:1], in_=inv_freq[:, 0:1], func=ACT.Abs_reciprocal_sqrt)
 
         x_codes = resident.tile([P, TOKEN_TILES, PASSES_A * P], U32, align_bytes=64)
         x_scales = resident.tile([P, TOKEN_TILES, PASSES_A * P], U8, align_bytes=64)
-        grouped_x = []
+        flipped_x = {}
+        grouped_x = {}
 
         def flip_hidden(tt):
             words = x_rows[tt][:].bitcast(F32)
-            grouped = stage.tile([P, PASSES_A * P * PACK], BF16, align_bytes=64, tag="grouped_x")
-            grouped_words = grouped[:].bitcast(F32).rearrange("p (g k u) -> p g k u", g=PASSES_A, u=2)
-            for ring, copy, first_pass in (
-                ("left", nc.scalar.copy, 0),
-                ("right", nc.vector.tensor_copy, 2),
-            ):
-                flipped = psum.tile([P, 2, 2, P], F32, tag=ring)
+            for half in range(2):
+                flipped_x[tt, half] = psum.tile([P, 2, 2, P], F32, name="flipped_x", tag="work", bufs=4)
                 for gg in range(2):
+                    first = (2 * half + gg) * (K_PASS // 2)
                     for u in range(2):
-                        first = (first_pass + gg) * (K_PASS // 2)
                         nc.tensor.transpose(
-                            flipped[:, gg, u, :],
+                            flipped_x[tt, half][:, gg, u, :],
                             words[:, first + u : first + K_PASS // 2 : 2],
                             ident_f32[:],
                         )
-                copy(
-                    out=grouped_words[:, first_pass : first_pass + 2, :, :],
-                    in_=flipped[:].rearrange("p g u k -> p g k u"),
-                )
-            grouped_x.append(grouped)
 
-        flip_hidden(0)
-        for tt in range(TOKEN_TILES):
-            if tt + 1 < TOKEN_TILES:
-                flip_hidden(tt + 1)
+        def regroup_hidden(tt, copies):
+            grouped_x[tt] = stage.tile(
+                [P, PASSES_A * P * PACK], BF16, align_bytes=64, name="grouped_x", tag="grouped_x"
+            )
+            grouped_words = grouped_x[tt][:].bitcast(F32).rearrange(
+                "p (g k u) -> p g k u", g=PASSES_A, u=2
+            )
+            for half, copy in enumerate(copies):
+                copy(
+                    out=grouped_words[:, 2 * half : 2 * half + 2, :, :],
+                    in_=flipped_x[tt, half][:].rearrange("p g u k -> p g k u"),
+                )
+
+        def quantise_hidden(tt):
             nc.vector.quantize_mx(
                 out=x_codes[:, tt, :].bitcast(FP8X4), scales=x_scales[:, tt, :], in_=grouped_x[tt][:]
             )
 
         a_codes = resident.tile([P, PASSES_A, FUSED], U32, align_bytes=64)
         a_scales = resident.tile([P, PASSES_A, FUSED], U8, align_bytes=64)
-        grouped_a = []
-        latent_ps = []
-        rope_ps = []
+        grouped_a = {}
+        latent_ps = {}
+        rope_ps = {}
 
         def regroup_a(g):
-            grouped = stage.tile(
-                [P, FUSED, PACK], BF16, align_bytes=64, tag="grouped_a", bufs=PASSES_A
+            grouped_a[g] = stage.tile(
+                [P, FUSED, PACK], BF16, align_bytes=64, name="grouped_a", tag="grouped_a"
             )
             for copy, cols in (
                 (nc.vector.tensor_copy, slice(0, A_SPLIT)),
                 (nc.scalar.copy, slice(A_SPLIT, FUSED)),
             ):
                 copy(
-                    out=grouped[:, cols, :].rearrange("p (c i) t -> p c t i", i=RUN),
+                    out=grouped_a[g][:, cols, :].rearrange("p (c i) t -> p c t i", i=RUN),
                     in_=raw_a[g][:, :, cols].rearrange("p t (c i) -> p c t i", i=RUN),
                 )
-            grouped_a.append(grouped)
 
         def quantise_a(g):
             for cols in (slice(0, LATENT), slice(LATENT, FUSED)):
@@ -197,59 +208,51 @@ def tile_mla_pb_kernel(tc, hidden_states, w_kv_a, kv_a_ln_w, w_kv_b, out_0, out_
                     in_=grouped_a[g][:, cols, :].rearrange("p c t -> p (c t)"),
                 )
 
-        def first_product(g):
+        def multiply_a(acc, tt, g, cols):
             of_pass = slice(g * P, (g + 1) * P)
-            for tt in range(TOKEN_TILES):
-                if g == 0:
-                    latent_ps.append(psum.tile([P, LATENT], F32, name="latent_ps", tag="left"))
-                    rope_ps.append(psum.tile([P, ROPE], F32, name="rope_ps", tag="right"))
-                for acc, cols in (
-                    (latent_ps[tt], slice(0, LATENT)),
-                    (rope_ps[tt], slice(LATENT, FUSED)),
-                ):
-                    nc.tensor.matmul_mx(
-                        out=acc[:],
-                        lhsT=x_codes[:, tt, of_pass].bitcast(FP8X4),
-                        lhsT_scale=x_scales[:, tt, of_pass],
-                        rhs=a_codes[:, g, cols].bitcast(FP8X4),
-                        rhs_scale=a_scales[:, g, cols],
-                        start=(g == 0),
-                        stop=(g == PASSES_A - 1),
-                    )
+            nc.tensor.matmul_mx(
+                out=acc[:],
+                lhsT=x_codes[:, tt, of_pass].bitcast(FP8X4),
+                lhsT_scale=x_scales[:, tt, of_pass],
+                rhs=a_codes[:, g, cols].bitcast(FP8X4),
+                rhs_scale=a_scales[:, g, cols],
+                start=(g == 0),
+                stop=(g == PASSES_A - 1),
+            )
 
-        regroup_a(0)
-        for g in range(PASSES_A):
-            if g + 1 < PASSES_A:
-                regroup_a(g + 1)
-            quantise_a(g)
-            first_product(g)
+        def latent_pass(tt, g):
+            if g == 0:
+                latent_ps[tt] = psum.tile([P, LATENT], F32, name="latent_ps", tag="latent")
+            multiply_a(latent_ps[tt], tt, g, slice(0, LATENT))
+
+        def rope_passes(tt):
+            rope_ps[tt] = psum.tile([P, ROPE], F32, name="rope_ps", tag="rope", bufs=1)
+            for g in range(PASSES_A):
+                multiply_a(rope_ps[tt], tt, g, slice(LATENT, FUSED))
 
         n_codes = resident.tile([P, TOKEN_TILES, P], U32, align_bytes=64)
         n_scales = resident.tile([P, TOKEN_TILES, P], U8, align_bytes=64)
         b_codes = resident.tile([P, PIECES, KINDS, BANK], U32, align_bytes=64)
         b_scales = resident.tile([P, PIECES, KINDS, BANK], U8, align_bytes=64)
+        gain = consts.tile([P, LATENT], BF16)
         kv_n = {}
         flipped_n = {}
         grouped_n = {}
         grouped_b = {}
-        k_pe = {}
         k_pieces = {}
 
         def sum_squares(tt):
-            squares = stage.tile([P, LATENT], BF16)
+            squares = stage.tile([P, LATENT], BF16, name="squares", tag="squares")
             nc.scalar.activation(
                 out=squares[:], in_=latent_ps[tt][:], func=ACT.Square,
                 accum_out=square_sum[:, tt : tt + 1],
             )
 
-        def root_mean_square(tt):
-            nc.scalar.activation(
-                out=rms[:, tt : tt + 1], in_=square_sum[:, tt : tt + 1], func=ACT.Sqrt,
-                bias=EPS, scale=1.0 / LATENT,
-            )
-
         def invert_rms(tt):
-            nc.vector.reciprocal(out=inv_rms[:, tt : tt + 1], in_=rms[:, tt : tt + 1])
+            nc.scalar.activation(
+                out=inv_rms[:, tt : tt + 1], in_=square_sum[:, tt : tt + 1],
+                func=ACT.Abs_reciprocal_sqrt, bias=EPS, scale=1.0 / LATENT,
+            )
 
         def normalise(tt):
             kv_n[tt] = stage.tile([P, LATENT], BF16, name="kv_n", tag="kv_n")
@@ -260,9 +263,11 @@ def tile_mla_pb_kernel(tc, hidden_states, w_kv_a, kv_a_ln_w, w_kv_b, out_0, out_
 
         def flip_kv_n(tt):
             words = kv_n[tt][:].bitcast(F32)
-            flipped_n[tt] = psum.tile([P, 2, P], F32, name="flipped_n", tag="right")
+            flipped_n[tt] = psum.tile([P, 2, P], F32, name="flipped_n", tag="kv_n_or_gain", bufs=1)
             for u in range(2):
                 nc.tensor.transpose(flipped_n[tt][:, u, :], words[:, u : K_PASS // 2 : 2], ident_f32[:])
+
+        def regroup_kv_n(tt):
             grouped_n[tt] = stage.tile(
                 [P, P * PACK], BF16, align_bytes=64, name="grouped_n", tag="grouped_n"
             )
@@ -273,9 +278,7 @@ def tile_mla_pb_kernel(tc, hidden_states, w_kv_a, kv_a_ln_w, w_kv_b, out_0, out_
 
         def quantise_kv_n(tt):
             nc.vector.quantize_mx(
-                out=n_codes[:, tt, :].bitcast(FP8X4),
-                scales=n_scales[:, tt, :],
-                in_=grouped_n[tt][:],
+                out=n_codes[:, tt, :].bitcast(FP8X4), scales=n_scales[:, tt, :], in_=grouped_n[tt][:]
             )
 
         def rotate(tt):
@@ -284,24 +287,23 @@ def tile_mla_pb_kernel(tc, hidden_states, w_kv_a, kv_a_ln_w, w_kv_b, out_0, out_
             a = tt % 2
             x1 = x[:, 0:HALF].unsqueeze(1).to_broadcast([P, 2, HALF])
             x2 = x[:, HALF:ROPE].unsqueeze(1).to_broadcast([P, 2, HALF])
-            from_x1 = stage.tile([P, 2, HALF], F32)
+            from_x1 = stage.tile([P, 2, HALF], F32, name="from_x1", tag="from_x1")
             nc.gpsimd.tensor_tensor(out=from_x1[:], in0=x1, in1=table[:, a, 1:3, :], op=ALU.mult)
-            from_x2 = stage.tile([P, 2, HALF], F32)
+            from_x2 = stage.tile([P, 2, HALF], F32, name="from_x2", tag="from_x2")
             nc.gpsimd.tensor_tensor(out=from_x2[:], in0=x2, in1=table[:, a, 0:2, :], op=ALU.mult)
-            k_pe[tt] = consts.tile([P, 2, HALF], F32, name="k_pe%d" % tt)
-            nc.gpsimd.tensor_tensor(out=k_pe[tt][:], in0=from_x1[:], in1=from_x2[:], op=ALU.add)
-
-        def spread_k_pe(j, tt):
-            k_pieces[j, tt] = pieces.tile(
-                [P, PIECE_HEADS, NOPE + ROPE], F32, name="k_piece", tag="k_piece"
-            )
-            nc.gpsimd.tensor_scalar(
-                out=k_pieces[j, tt][:, :, NOPE:],
-                in0=k_pe[tt][:].rearrange("p h c -> p (h c)").unsqueeze(1).to_broadcast(
-                    [P, PIECE_HEADS, ROPE]
-                ),
-                scalar1=1.0, scalar2=0.0, op0=ALU.mult, op1=ALU.add,
-            )
+            k_pe = stage.tile([P, 2, HALF], F32, name="k_pe", tag="k_pe")
+            nc.gpsimd.tensor_tensor(out=k_pe[:], in0=from_x1[:], in1=from_x2[:], op=ALU.add)
+            for i in range(KEY_TILES):
+                k_pieces[tt, i] = resident.tile(
+                    [P, PIECE_HEADS, NOPE + ROPE], F32, name="k_piece%d_%d" % (tt, i)
+                )
+                nc.gpsimd.tensor_scalar(
+                    out=k_pieces[tt, i][:, :, NOPE:],
+                    in0=k_pe[:].rearrange("p h c -> p (h c)").unsqueeze(1).to_broadcast(
+                        [P, PIECE_HEADS, ROPE]
+                    ),
+                    scalar1=1.0, scalar2=0.0, op0=ALU.mult, op1=ALU.add,
+                )
 
         def regroup_b(j, kind):
             grouped_b[j, kind] = stage.tile(
@@ -310,10 +312,13 @@ def tile_mla_pb_kernel(tc, hidden_states, w_kv_a, kv_a_ln_w, w_kv_b, out_0, out_
             by_kind = raw_b[j][:].rearrange(
                 "p t (h s c i) -> p s h c t i", h=PIECE_HEADS, s=KINDS, i=RUN
             )
-            nc.vector.tensor_copy(
-                out=grouped_b[j, kind][:].rearrange("p (h c i) t -> p h c t i", h=PIECE_HEADS, i=RUN),
-                in_=by_kind[:, kind],
-            )
+            by_run = grouped_b[j, kind][:].rearrange("p (h c i) t -> p h c t i", h=PIECE_HEADS, i=RUN)
+            for copy, runs in (
+                (nc.vector.tensor_copy, slice(0, B_SPLIT // RUN)),
+                (nc.scalar.copy, slice(B_SPLIT // RUN, NOPE // RUN)),
+            ):
+                for_kind = by_kind[:, kind]
+                copy(out=by_run[:, :, runs], in_=for_kind[:, :, runs])
 
         def quantise_b(j, kind):
             nc.vector.quantize_mx(
@@ -322,8 +327,8 @@ def tile_mla_pb_kernel(tc, hidden_states, w_kv_a, kv_a_ln_w, w_kv_b, out_0, out_
                 in_=grouped_b[j, kind][:].rearrange("p c t -> p (c t)"),
             )
 
-        def multiply_b(j, tt, kind, ring):
-            kv_ps = psum.tile([P, BANK], F32, name="kv_ps", tag=ring)
+        def multiply_b(j, tt, kind):
+            kv_ps = psum.tile([P, BANK], F32, name="kv_ps", tag="work", bufs=4)
             nc.tensor.matmul_mx(
                 out=kv_ps[:],
                 lhsT=n_codes[:, tt, :].bitcast(FP8X4),
@@ -335,47 +340,77 @@ def tile_mla_pb_kernel(tc, hidden_states, w_kv_a, kv_a_ln_w, w_kv_b, out_0, out_
             )
             return kv_ps[:].rearrange("p (h c) -> p h c", h=PIECE_HEADS)
 
-        def second_product(j, tt):
-            if j + 1 < PIECES:
-                if tt % 2 == 0:
-                    regroup_b(j + 1, tt // 2)
-                else:
-                    quantise_b(j + 1, tt // 2)
+        def keys(j, tt):
             tokens = slice(tt * P, (tt + 1) * P)
             heads = slice(j * PIECE_HEADS, (j + 1) * PIECE_HEADS)
-            nc.scalar.copy(out=k_pieces[j, tt][:, :, :NOPE], in_=multiply_b(j, tt, KIND_K_NOPE, "left"))
-            nc.sync.dma_start(out=k_out[tokens, heads, :], in_=k_pieces[j, tt][:])
-            v_piece = pieces.tile([P, PIECE_HEADS, V_DIM], F32)
-            copy = nc.vector.tensor_copy if tt % 2 == 1 else nc.scalar.copy
-            copy(out=v_piece[:], in_=multiply_b(j, tt, KIND_V, "right"))
+            piece = k_pieces[tt, j % KEY_TILES]
+            nc.scalar.copy(out=piece[:, :, :NOPE], in_=multiply_b(j, tt, KIND_K_NOPE))
+            nc.sync.dma_start(out=k_out[tokens, heads, :], in_=piece[:])
+
+        def values(j, tt):
+            tokens = slice(tt * P, (tt + 1) * P)
+            heads = slice(j * PIECE_HEADS, (j + 1) * PIECE_HEADS)
+            v_piece = pieces.tile([P, PIECE_HEADS, V_DIM], F32, name="v_piece", tag="v_piece")
+            nc.scalar.copy(out=v_piece[:], in_=multiply_b(j, tt, KIND_V))
             nc.sync.dma_start(out=v_out[tokens, heads, :], in_=v_piece[:])
 
-        for kind in range(KINDS):
-            regroup_b(0, kind)
-        for kind in range(KINDS):
-            quantise_b(0, kind)
+        flip_hidden(0)
+        regroup_hidden(0, (nc.scalar.copy, nc.vector.tensor_copy))
+        gain_ps = psum.tile([P, LATENT], F32, name="gain_ps", tag="kv_n_or_gain", bufs=1)
+        nc.tensor.matmul(out=gain_ps[:], lhsT=ones[:], rhs=gain_row[:], start=True, stop=True)
+        regroup_a(0)
+        quantise_hidden(0)
+        for g in range(PASSES_A):
+            if g + 1 < PASSES_A:
+                regroup_a(g + 1)
+            quantise_a(g)
+            if g > 1:
+                flip_hidden(g - 1)
+            latent_pass(0, g)
+        rope_passes(0)
+        regroup_hidden(1, (nc.scalar.copy, nc.scalar.copy))
+        nc.scalar.copy(out=gain[:], in_=gain_ps[:])
 
         def is_tile(tt):
             return 0 <= tt < TOKEN_TILES
 
-        for step in range(TOKEN_TILES + 4):
+        for step in range(TOKEN_TILES + 2):
             if is_tile(step - 1):
-                invert_rms(step - 1)
-            if is_tile(step - 3):
-                quantise_kv_n(step - 3)
-            if is_tile(step - 1):
-                normalise(step - 1)
-            if is_tile(step - 4):
-                second_product(0, step - 4)
+                flip_kv_n(step - 1)
             if is_tile(step):
                 sum_squares(step)
+                invert_rms(step)
                 rotate(step)
-                spread_k_pe(0, step)
-                root_mean_square(step)
             if is_tile(step - 2):
-                flip_kv_n(step - 2)
+                keys(0, step - 2)
+            if is_tile(step - 1):
+                regroup_kv_n(step - 1)
+            if is_tile(step - 2):
+                values(0, step - 2)
+            if is_tile(step + 1):
+                quantise_hidden(step + 1)
+            if is_tile(step):
+                regroup_b(step // KINDS, step % KINDS)
+                normalise(step)
+            if is_tile(step - 1):
+                quantise_kv_n(step - 1)
+            if is_tile(step):
+                quantise_b(step // KINDS, step % KINDS)
+            if is_tile(step + 1):
+                for g in range(PASSES_A):
+                    latent_pass(step + 1, g)
+                rope_passes(step + 1)
+            if is_tile(step + 2):
+                regroup_hidden(step + 2, (nc.scalar.copy, nc.scalar.copy))
+            if step + 3 == TOKEN_TILES - 1:
+                flip_hidden(step + 3)
 
         for j in range(1, PIECES):
             for tt in range(TOKEN_TILES):
-                spread_k_pe(j, tt)
-                second_product(j, tt)
+                if j + 1 < PIECES:
+                    if tt % 2 == 0:
+                        regroup_b(j + 1, tt // 2)
+                    else:
+                        quantise_b(j + 1, tt // 2)
+                keys(j, tt)
+                values(j, tt)

@@ -123,7 +123,7 @@ def tile_mla_pb_kernel(tc, hidden_states, w_kv_a, kv_a_ln_w, w_kv_b, out_0, out_
             out=position_turns[:], in0=position[:], scalar1=1.0 / (2.0 * math.pi), scalar2=None,
             op0=ALU.mult,
         )
-        phases = (0.5, 0.25, 0.0)
+        phases = (0.25, 0.0)
         turns = consts.tile([P, 2, len(phases), HALF], F32)
         for a in range(2):
             for i, phase in enumerate(phases):
@@ -138,8 +138,13 @@ def tile_mla_pb_kernel(tc, hidden_states, w_kv_a, kv_a_ln_w, w_kv_b, out_0, out_
         )
         part_turns = consts.tile([P, 2, len(phases), HALF], F32)
         nc.vector.tensor_tensor(out=part_turns[:], in0=turns[:], in1=whole_turns[:], op=ALU.subtract)
-        table = consts.tile([P, 2, len(phases), HALF], F32)
-        nc.scalar.activation(out=table[:], in_=part_turns[:], func=ACT.Sin, scale=2.0 * math.pi)
+        table = consts.tile([P, 2, len(phases) + 1, HALF], F32)
+        nc.scalar.activation(
+            out=table[:, :, 1:3, :], in_=part_turns[:], func=ACT.Sin, scale=2.0 * math.pi
+        )
+        nc.scalar.activation(
+            out=table[:, :, 0, :], in_=part_turns[:, :, 1, :], func=ACT.Sin, scale=-2.0 * math.pi
+        )
 
         square_sum = consts.tile([P, TOKEN_TILES], F32)
         inv_rms = consts.tile([P, TOKEN_TILES], F32)
@@ -239,7 +244,9 @@ def tile_mla_pb_kernel(tc, hidden_states, w_kv_a, kv_a_ln_w, w_kv_b, out_0, out_
         flipped_n = {}
         grouped_n = {}
         grouped_b = {}
+        k_pe = {}
         k_pieces = {}
+        kv_ps = {}
 
         def sum_squares(tt):
             squares = stage.tile([P, LATENT], BF16, name="squares", tag="squares")
@@ -282,27 +289,26 @@ def tile_mla_pb_kernel(tc, hidden_states, w_kv_a, kv_a_ln_w, w_kv_b, out_0, out_
             )
 
         def rotate(tt):
-            x = stage.tile([P, ROPE], F32, name="rope_x", tag="rope_x")
-            nc.scalar.copy(out=x[:], in_=rope_ps[tt][:])
             a = tt % 2
-            x1 = x[:, 0:HALF].unsqueeze(1).to_broadcast([P, 2, HALF])
-            x2 = x[:, HALF:ROPE].unsqueeze(1).to_broadcast([P, 2, HALF])
+            x1 = rope_ps[tt][:, 0:HALF].unsqueeze(1).to_broadcast([P, 2, HALF])
+            x2 = rope_ps[tt][:, HALF:ROPE].unsqueeze(1).to_broadcast([P, 2, HALF])
             from_x1 = stage.tile([P, 2, HALF], F32, name="from_x1", tag="from_x1")
-            nc.gpsimd.tensor_tensor(out=from_x1[:], in0=x1, in1=table[:, a, 1:3, :], op=ALU.mult)
+            nc.vector.tensor_tensor(out=from_x1[:], in0=x1, in1=table[:, a, 1:3, :], op=ALU.mult)
             from_x2 = stage.tile([P, 2, HALF], F32, name="from_x2", tag="from_x2")
-            nc.gpsimd.tensor_tensor(out=from_x2[:], in0=x2, in1=table[:, a, 0:2, :], op=ALU.mult)
-            k_pe = stage.tile([P, 2, HALF], F32, name="k_pe", tag="k_pe")
-            nc.gpsimd.tensor_tensor(out=k_pe[:], in0=from_x1[:], in1=from_x2[:], op=ALU.add)
+            nc.vector.tensor_tensor(out=from_x2[:], in0=x2, in1=table[:, a, 0:2, :], op=ALU.mult)
+            k_pe[tt] = stage.tile([P, 2, HALF], F32, name="k_pe", tag="k_pe")
+            nc.vector.tensor_tensor(out=k_pe[tt][:], in0=from_x1[:], in1=from_x2[:], op=ALU.add)
+
+        def spread_k_pe(tt):
             for i in range(KEY_TILES):
                 k_pieces[tt, i] = resident.tile(
                     [P, PIECE_HEADS, NOPE + ROPE], F32, name="k_piece%d_%d" % (tt, i)
                 )
-                nc.gpsimd.tensor_scalar(
+                nc.vector.tensor_copy(
                     out=k_pieces[tt, i][:, :, NOPE:],
-                    in0=k_pe[:].rearrange("p h c -> p (h c)").unsqueeze(1).to_broadcast(
+                    in_=k_pe[tt][:].rearrange("p h c -> p (h c)").unsqueeze(1).to_broadcast(
                         [P, PIECE_HEADS, ROPE]
                     ),
-                    scalar1=1.0, scalar2=0.0, op0=ALU.mult, op1=ALU.add,
                 )
 
         def regroup_b(j, kind):
@@ -328,9 +334,9 @@ def tile_mla_pb_kernel(tc, hidden_states, w_kv_a, kv_a_ln_w, w_kv_b, out_0, out_
             )
 
         def multiply_b(j, tt, kind):
-            kv_ps = psum.tile([P, BANK], F32, name="kv_ps", tag="work", bufs=4)
+            kv_ps[j, tt, kind] = psum.tile([P, BANK], F32, name="kv_ps", tag="work", bufs=4)
             nc.tensor.matmul_mx(
-                out=kv_ps[:],
+                out=kv_ps[j, tt, kind][:],
                 lhsT=n_codes[:, tt, :].bitcast(FP8X4),
                 lhsT_scale=n_scales[:, tt, :],
                 rhs=b_codes[:, j, kind, :].bitcast(FP8X4),
@@ -338,24 +344,26 @@ def tile_mla_pb_kernel(tc, hidden_states, w_kv_a, kv_a_ln_w, w_kv_b, out_0, out_
                 start=True,
                 stop=True,
             )
-            return kv_ps[:].rearrange("p (h c) -> p h c", h=PIECE_HEADS)
 
-        def keys(j, tt):
+        def by_head(j, tt, kind):
+            return kv_ps[j, tt, kind][:].rearrange("p (h c) -> p h c", h=PIECE_HEADS)
+
+        def store_keys(j, tt):
             tokens = slice(tt * P, (tt + 1) * P)
             heads = slice(j * PIECE_HEADS, (j + 1) * PIECE_HEADS)
             piece = k_pieces[tt, j % KEY_TILES]
-            nc.scalar.copy(out=piece[:, :, :NOPE], in_=multiply_b(j, tt, KIND_K_NOPE))
+            nc.scalar.copy(out=piece[:, :, :NOPE], in_=by_head(j, tt, KIND_K_NOPE))
             nc.sync.dma_start(out=k_out[tokens, heads, :], in_=piece[:])
 
-        def values(j, tt):
+        def store_values(j, tt, copy):
             tokens = slice(tt * P, (tt + 1) * P)
             heads = slice(j * PIECE_HEADS, (j + 1) * PIECE_HEADS)
             v_piece = pieces.tile([P, PIECE_HEADS, V_DIM], F32, name="v_piece", tag="v_piece")
-            nc.scalar.copy(out=v_piece[:], in_=multiply_b(j, tt, KIND_V))
+            copy(out=v_piece[:], in_=by_head(j, tt, KIND_V))
             nc.sync.dma_start(out=v_out[tokens, heads, :], in_=v_piece[:])
 
         flip_hidden(0)
-        regroup_hidden(0, (nc.scalar.copy, nc.vector.tensor_copy))
+        regroup_hidden(0, (nc.vector.tensor_copy, nc.vector.tensor_copy))
         gain_ps = psum.tile([P, LATENT], F32, name="gain_ps", tag="kv_n_or_gain", bufs=1)
         nc.tensor.matmul(out=gain_ps[:], lhsT=ones[:], rhs=gain_row[:], start=True, stop=True)
         regroup_a(0)
@@ -374,28 +382,40 @@ def tile_mla_pb_kernel(tc, hidden_states, w_kv_a, kv_a_ln_w, w_kv_b, out_0, out_
         def is_tile(tt):
             return 0 <= tt < TOKEN_TILES
 
-        for step in range(TOKEN_TILES + 2):
+        regroup_in_step = {0: (0, KIND_K_NOPE), 1: (0, KIND_V), 3: (1, KIND_K_NOPE), 4: (1, KIND_V)}
+        quantise_in_step = {0: (0, KIND_K_NOPE), 2: (0, KIND_V), 4: (1, KIND_K_NOPE), 5: (1, KIND_V)}
+
+        for step in range(TOKEN_TILES + 3):
+            if is_tile(step - 2):
+                multiply_b(0, step - 2, KIND_K_NOPE)
             if is_tile(step - 1):
                 flip_kv_n(step - 1)
+            if is_tile(step - 3):
+                multiply_b(0, step - 3, KIND_V)
             if is_tile(step):
                 sum_squares(step)
-                invert_rms(step)
-                rotate(step)
-            if is_tile(step - 2):
-                keys(0, step - 2)
             if is_tile(step - 1):
                 regroup_kv_n(step - 1)
+            if is_tile(step):
+                invert_rms(step)
             if is_tile(step - 2):
-                values(0, step - 2)
+                store_keys(0, step - 2)
+            if is_tile(step - 3):
+                store_values(0, step - 3, nc.scalar.copy)
             if is_tile(step + 1):
                 quantise_hidden(step + 1)
             if is_tile(step):
-                regroup_b(step // KINDS, step % KINDS)
-                normalise(step)
+                rotate(step)
             if is_tile(step - 1):
                 quantise_kv_n(step - 1)
+            if step in regroup_in_step:
+                regroup_b(*regroup_in_step[step])
             if is_tile(step):
-                quantise_b(step // KINDS, step % KINDS)
+                normalise(step)
+            if step in quantise_in_step:
+                quantise_b(*quantise_in_step[step])
+            if is_tile(step):
+                spread_k_pe(step)
             if is_tile(step + 1):
                 for g in range(PASSES_A):
                     latent_pass(step + 1, g)
@@ -412,5 +432,7 @@ def tile_mla_pb_kernel(tc, hidden_states, w_kv_a, kv_a_ln_w, w_kv_b, out_0, out_
                         regroup_b(j + 1, tt // 2)
                     else:
                         quantise_b(j + 1, tt // 2)
-                keys(j, tt)
-                values(j, tt)
+                for kind in range(KINDS):
+                    multiply_b(j, tt, kind)
+                store_keys(j, tt)
+                store_values(j, tt, nc.vector.tensor_copy if tt % 2 == 1 else nc.scalar.copy)

@@ -44,7 +44,7 @@ PIECES = HEADS // PIECE_HEADS
 KEY_TILES = 2
 
 RUN = 4
-B_SPLIT = 96
+B_SPLIT = (96, 96, 128, 128)
 A_SPLIT = FUSED // 2
 
 ROUND_MAGIC = 1.5 * 2.0**23
@@ -93,17 +93,15 @@ def tile_mla_pb_kernel(tc, hidden_states, w_kv_a, kv_a_ln_w, w_kv_b, out_0, out_
         ident_f32 = consts.tile([P, P], F32)
         make_identity(nc, ident_f32[:])
         nc.gpsimd.memset(gain_row[:], 0.0)
-        ones = consts.tile([P, P], BF16)
+        ones = consts.tile([P, BANK], BF16)
         nc.gpsimd.memset(ones[:], 1.0)
         load_x(0)
-        load_gain()
         for g in range(PASSES_A):
             load_a(g)
-        load_x(1)
-        load_x(2)
-        load_b(0)
-        load_x(3)
-        for j in range(1, PIECES):
+        load_gain()
+        for tt in range(1, TOKEN_TILES):
+            load_x(tt)
+        for j in range(PIECES):
             load_b(j)
 
         warm = consts.tile([P, 1], F32)
@@ -112,32 +110,36 @@ def tile_mla_pb_kernel(tc, hidden_states, w_kv_a, kv_a_ln_w, w_kv_b, out_0, out_
         nc.scalar.activation(out=warm_out[:], in_=warm[:], func=ACT.Sin)
         inv_freq = consts.tile([P, HALF], F32)
         nc.vector.memset(inv_freq[:, 0:1], 1.0)
-        for level in range(HALF_LOG2):
-            width = 2**level
-            nc.vector.tensor_scalar(
-                out=inv_freq[:, width : 2 * width], in0=inv_freq[:, 0:width],
-                scalar1=ROPE_BASE ** (-width / HALF), scalar2=None, op0=ALU.mult,
-            )
         position_turns = consts.tile([P, 2], F32)
         nc.vector.tensor_scalar(
             out=position_turns[:], in0=position[:], scalar1=1.0 / (2.0 * math.pi), scalar2=None,
             op0=ALU.mult,
         )
+        for width in (1, 4, 16):
+            for first in range(width, 4 * width, width):
+                nc.vector.tensor_scalar(
+                    out=inv_freq[:, first : first + width], in0=inv_freq[:, 0:width],
+                    scalar1=ROPE_BASE ** (-first / HALF), scalar2=None, op0=ALU.mult,
+                )
         phases = (0.25, 0.0)
         turns = consts.tile([P, 2, len(phases), HALF], F32)
+        whole_turns = consts.tile([P, 2, len(phases), HALF], F32)
+        part_turns = consts.tile([P, 2, len(phases), HALF], F32)
         for a in range(2):
             for i, phase in enumerate(phases):
                 nc.vector.tensor_scalar(
                     out=turns[:, a, i, :], in0=inv_freq[:], scalar1=position_turns[:, a : a + 1],
                     scalar2=phase, op0=ALU.mult, op1=ALU.add,
                 )
-        whole_turns = consts.tile([P, 2, len(phases), HALF], F32)
-        nc.vector.tensor_scalar(
-            out=whole_turns[:], in0=turns[:], scalar1=ROUND_MAGIC, scalar2=ROUND_MAGIC,
-            op0=ALU.add, op1=ALU.subtract,
-        )
-        part_turns = consts.tile([P, 2, len(phases), HALF], F32)
-        nc.vector.tensor_tensor(out=part_turns[:], in0=turns[:], in1=whole_turns[:], op=ALU.subtract)
+        for a in range(2):
+            nc.vector.tensor_scalar(
+                out=whole_turns[:, a], in0=turns[:, a], scalar1=ROUND_MAGIC, scalar2=ROUND_MAGIC,
+                op0=ALU.add, op1=ALU.subtract,
+            )
+        for a in range(2):
+            nc.vector.tensor_tensor(
+                out=part_turns[:, a], in0=turns[:, a], in1=whole_turns[:, a], op=ALU.subtract
+            )
         table = consts.tile([P, 2, len(phases) + 1, HALF], F32)
         nc.scalar.activation(
             out=table[:, :, 1:3, :], in_=part_turns[:], func=ACT.Sin, scale=2.0 * math.pi
@@ -194,7 +196,8 @@ def tile_mla_pb_kernel(tc, hidden_states, w_kv_a, kv_a_ln_w, w_kv_b, out_0, out_
 
         def regroup_a(g):
             grouped_a[g] = stage.tile(
-                [P, FUSED, PACK], BF16, align_bytes=64, name="grouped_a", tag="grouped_a"
+                [P, FUSED, PACK], BF16, align_bytes=64, name="grouped_a", tag="grouped_a",
+                bufs=PASSES_A,
             )
             for copy, cols in (
                 (nc.vector.tensor_copy, slice(0, A_SPLIT)),
@@ -244,6 +247,7 @@ def tile_mla_pb_kernel(tc, hidden_states, w_kv_a, kv_a_ln_w, w_kv_b, out_0, out_
         flipped_n = {}
         grouped_n = {}
         grouped_b = {}
+        rotated = {}
         k_pe = {}
         k_pieces = {}
         kv_ps = {}
@@ -296,20 +300,23 @@ def tile_mla_pb_kernel(tc, hidden_states, w_kv_a, kv_a_ln_w, w_kv_b, out_0, out_
             nc.vector.tensor_tensor(out=from_x1[:], in0=x1, in1=table[:, a, 1:3, :], op=ALU.mult)
             from_x2 = stage.tile([P, 2, HALF], F32, name="from_x2", tag="from_x2")
             nc.vector.tensor_tensor(out=from_x2[:], in0=x2, in1=table[:, a, 0:2, :], op=ALU.mult)
-            k_pe[tt] = stage.tile([P, 2, HALF], F32, name="k_pe", tag="k_pe")
+            rotated[tt] = (from_x1, from_x2)
+
+        def add_k_pe(tt):
+            k_pe[tt] = resident.tile([P, 2, HALF], F32, name="k_pe%d" % tt)
+            from_x1, from_x2 = rotated[tt]
             nc.vector.tensor_tensor(out=k_pe[tt][:], in0=from_x1[:], in1=from_x2[:], op=ALU.add)
 
-        def spread_k_pe(tt):
-            for i in range(KEY_TILES):
-                k_pieces[tt, i] = resident.tile(
-                    [P, PIECE_HEADS, NOPE + ROPE], F32, name="k_piece%d_%d" % (tt, i)
-                )
-                nc.vector.tensor_copy(
-                    out=k_pieces[tt, i][:, :, NOPE:],
-                    in_=k_pe[tt][:].rearrange("p h c -> p (h c)").unsqueeze(1).to_broadcast(
-                        [P, PIECE_HEADS, ROPE]
-                    ),
-                )
+        def spread_k_pe(tt, i):
+            k_pieces[tt, i] = resident.tile(
+                [P, PIECE_HEADS, NOPE + ROPE], F32, name="k_piece%d_%d" % (tt, i)
+            )
+            nc.vector.tensor_copy(
+                out=k_pieces[tt, i][:, :, NOPE:],
+                in_=k_pe[tt][:].rearrange("p h c -> p (h c)").unsqueeze(1).to_broadcast(
+                    [P, PIECE_HEADS, ROPE]
+                ),
+            )
 
         def regroup_b(j, kind):
             grouped_b[j, kind] = stage.tile(
@@ -318,13 +325,15 @@ def tile_mla_pb_kernel(tc, hidden_states, w_kv_a, kv_a_ln_w, w_kv_b, out_0, out_
             by_kind = raw_b[j][:].rearrange(
                 "p t (h s c i) -> p s h c t i", h=PIECE_HEADS, s=KINDS, i=RUN
             )
+            vector_cols = B_SPLIT[j]
             by_run = grouped_b[j, kind][:].rearrange("p (h c i) t -> p h c t i", h=PIECE_HEADS, i=RUN)
             for copy, runs in (
-                (nc.vector.tensor_copy, slice(0, B_SPLIT // RUN)),
-                (nc.scalar.copy, slice(B_SPLIT // RUN, NOPE // RUN)),
+                (nc.vector.tensor_copy, slice(0, vector_cols // RUN)),
+                (nc.scalar.copy, slice(vector_cols // RUN, NOPE // RUN)),
             ):
-                for_kind = by_kind[:, kind]
-                copy(out=by_run[:, :, runs], in_=for_kind[:, :, runs])
+                if runs.start < runs.stop:
+                    for_kind = by_kind[:, kind]
+                    copy(out=by_run[:, :, runs], in_=for_kind[:, :, runs])
 
         def quantise_b(j, kind):
             nc.vector.quantize_mx(
@@ -362,68 +371,82 @@ def tile_mla_pb_kernel(tc, hidden_states, w_kv_a, kv_a_ln_w, w_kv_b, out_0, out_
             copy(out=v_piece[:], in_=by_head(j, tt, KIND_V))
             nc.sync.dma_start(out=v_out[tokens, heads, :], in_=v_piece[:])
 
+        def keep_warm(count):
+            for i in range(count):
+                unread = psum.tile([P, BANK], F32, name="unread", tag="kv_n_or_gain", bufs=1)
+                nc.tensor.matmul(out=unread[:], lhsT=ones[:, 0:P], rhs=ones[:], start=True, stop=True)
+
+        keep_warm(4)
         flip_hidden(0)
+        keep_warm(6)
         regroup_hidden(0, (nc.vector.tensor_copy, nc.vector.tensor_copy))
-        gain_ps = psum.tile([P, LATENT], F32, name="gain_ps", tag="kv_n_or_gain", bufs=1)
-        nc.tensor.matmul(out=gain_ps[:], lhsT=ones[:], rhs=gain_row[:], start=True, stop=True)
         regroup_a(0)
         quantise_hidden(0)
         for g in range(PASSES_A):
             if g + 1 < PASSES_A:
                 regroup_a(g + 1)
             quantise_a(g)
-            if g > 1:
-                flip_hidden(g - 1)
             latent_pass(0, g)
-        rope_passes(0)
+            if g == 0:
+                keep_warm(2)
+            if g == 1:
+                flip_hidden(1)
+            if g == 2:
+                keep_warm(1)
+        gain_ps = psum.tile([P, LATENT], F32, name="gain_ps", tag="kv_n_or_gain", bufs=1)
+        nc.tensor.matmul(out=gain_ps[:], lhsT=ones[:, 0:P], rhs=gain_row[:], start=True, stop=True)
         regroup_hidden(1, (nc.scalar.copy, nc.scalar.copy))
+        rope_passes(0)
+        flip_hidden(2)
+        sum_squares(0)
         nc.scalar.copy(out=gain[:], in_=gain_ps[:])
+        invert_rms(0)
+        quantise_hidden(1)
+        rotate(0)
+        normalise(0)
+        add_k_pe(0)
 
         def is_tile(tt):
             return 0 <= tt < TOKEN_TILES
 
-        regroup_in_step = {0: (0, KIND_K_NOPE), 1: (0, KIND_V), 3: (1, KIND_K_NOPE), 4: (1, KIND_V)}
-        quantise_in_step = {0: (0, KIND_K_NOPE), 2: (0, KIND_V), 4: (1, KIND_K_NOPE), 5: (1, KIND_V)}
-
-        for step in range(TOKEN_TILES + 3):
-            if is_tile(step - 2):
-                multiply_b(0, step - 2, KIND_K_NOPE)
-            if is_tile(step - 1):
-                flip_kv_n(step - 1)
-            if is_tile(step - 3):
-                multiply_b(0, step - 3, KIND_V)
-            if is_tile(step):
-                sum_squares(step)
-            if is_tile(step - 1):
-                regroup_kv_n(step - 1)
-            if is_tile(step):
-                invert_rms(step)
-            if is_tile(step - 2):
-                store_keys(0, step - 2)
-            if is_tile(step - 3):
-                store_values(0, step - 3, nc.scalar.copy)
-            if is_tile(step + 1):
-                quantise_hidden(step + 1)
-            if is_tile(step):
-                rotate(step)
-            if is_tile(step - 1):
-                quantise_kv_n(step - 1)
-            if step in regroup_in_step:
-                regroup_b(*regroup_in_step[step])
-            if is_tile(step):
-                normalise(step)
-            if step in quantise_in_step:
-                quantise_b(*quantise_in_step[step])
-            if is_tile(step):
-                spread_k_pe(step)
+        for step in range(TOKEN_TILES + 2):
+            if is_tile(step + 2):
+                regroup_hidden(step + 2, (nc.scalar.copy, nc.scalar.copy))
+                quantise_hidden(step + 2)
+            if step < KINDS:
+                regroup_b(0, step)
             if is_tile(step + 1):
                 for g in range(PASSES_A):
                     latent_pass(step + 1, g)
+                sum_squares(step + 1)
+            if is_tile(step - 1):
+                multiply_b(0, step - 1, KIND_K_NOPE)
+                store_keys(0, step - 1)
+            if is_tile(step):
+                flip_kv_n(step)
+                regroup_kv_n(step)
+                quantise_kv_n(step)
+            if is_tile(step + 1):
+                invert_rms(step + 1)
+                normalise(step + 1)
                 rope_passes(step + 1)
-            if is_tile(step + 2):
-                regroup_hidden(step + 2, (nc.scalar.copy, nc.scalar.copy))
-            if step + 3 == TOKEN_TILES - 1:
+            if is_tile(step + 3):
                 flip_hidden(step + 3)
+            if step < KINDS:
+                quantise_b(0, step)
+            if is_tile(step):
+                spread_k_pe(step, 0)
+            if is_tile(step + 1):
+                rotate(step + 1)
+                add_k_pe(step + 1)
+            if step >= TOKEN_TILES - 1:
+                if step - TOKEN_TILES + 1 < KINDS:
+                    regroup_b(1, step - TOKEN_TILES + 1)
+                if step - TOKEN_TILES >= 0:
+                    quantise_b(1, step - TOKEN_TILES)
+            if is_tile(step - 2):
+                multiply_b(0, step - 2, KIND_V)
+                store_values(0, step - 2, nc.scalar.copy)
 
         for j in range(1, PIECES):
             for tt in range(TOKEN_TILES):
@@ -432,6 +455,8 @@ def tile_mla_pb_kernel(tc, hidden_states, w_kv_a, kv_a_ln_w, w_kv_b, out_0, out_
                         regroup_b(j + 1, tt // 2)
                     else:
                         quantise_b(j + 1, tt // 2)
+                if j == 1:
+                    spread_k_pe(tt, 1)
                 for kind in range(KINDS):
                     multiply_b(j, tt, kind)
                 store_keys(j, tt)

@@ -45,7 +45,7 @@ KEY_TILES = 2
 
 RUN = 4
 B_SPLIT = (96, 96, 128, 128)
-A_SPLIT = FUSED // 2
+A_SPLIT = 304
 
 ROUND_MAGIC = 1.5 * 2.0**23
 
@@ -94,7 +94,7 @@ def tile_mla_pb_kernel(tc, hidden_states, w_kv_a, kv_a_ln_w, w_kv_b, out_0, out_
         make_identity(nc, ident_f32[:])
         nc.gpsimd.memset(gain_row[:], 0.0)
         ones = consts.tile([P, BANK], BF16)
-        nc.gpsimd.memset(ones[:], 1.0)
+        nc.vector.memset(ones[:], 1.0)
         load_x(0)
         for g in range(PASSES_A):
             load_a(g)
@@ -108,39 +108,33 @@ def tile_mla_pb_kernel(tc, hidden_states, w_kv_a, kv_a_ln_w, w_kv_b, out_0, out_
         nc.vector.memset(warm[:], 0.0)
         warm_out = consts.tile([P, 1], F32)
         nc.scalar.activation(out=warm_out[:], in_=warm[:], func=ACT.Sin)
-        inv_freq = consts.tile([P, HALF], F32)
-        nc.vector.memset(inv_freq[:, 0:1], 1.0)
-        position_turns = consts.tile([P, 2], F32)
+        turns = consts.tile([P, 2, 2, HALF], F32)
+        whole_turns = consts.tile([P, 2, 2, HALF], F32)
+        part_turns = consts.tile([P, 2, 2, HALF], F32)
         nc.vector.tensor_scalar(
-            out=position_turns[:], in0=position[:], scalar1=1.0 / (2.0 * math.pi), scalar2=None,
-            op0=ALU.mult,
+            out=turns[:, :, 1, 0:1], in0=position[:].unsqueeze(2), scalar1=1.0 / (2.0 * math.pi),
+            scalar2=None, op0=ALU.mult,
         )
         for width in (1, 4, 16):
             for first in range(width, 4 * width, width):
                 nc.vector.tensor_scalar(
-                    out=inv_freq[:, first : first + width], in0=inv_freq[:, 0:width],
+                    out=turns[:, :, 1, first : first + width], in0=turns[:, :, 1, 0:width],
                     scalar1=ROPE_BASE ** (-first / HALF), scalar2=None, op0=ALU.mult,
                 )
-        phases = (0.25, 0.0)
-        turns = consts.tile([P, 2, len(phases), HALF], F32)
-        whole_turns = consts.tile([P, 2, len(phases), HALF], F32)
-        part_turns = consts.tile([P, 2, len(phases), HALF], F32)
-        for a in range(2):
-            for i, phase in enumerate(phases):
-                nc.vector.tensor_scalar(
-                    out=turns[:, a, i, :], in0=inv_freq[:], scalar1=position_turns[:, a : a + 1],
-                    scalar2=phase, op0=ALU.mult, op1=ALU.add,
-                )
-        for a in range(2):
+        nc.vector.tensor_scalar(
+            out=turns[:, :, 0, :], in0=turns[:, :, 1, :], scalar1=0.25, scalar2=None, op0=ALU.add,
+        )
+        for i in (1, 0):
             nc.vector.tensor_scalar(
-                out=whole_turns[:, a], in0=turns[:, a], scalar1=ROUND_MAGIC, scalar2=ROUND_MAGIC,
-                op0=ALU.add, op1=ALU.subtract,
+                out=whole_turns[:, :, i], in0=turns[:, :, i], scalar1=ROUND_MAGIC,
+                scalar2=ROUND_MAGIC, op0=ALU.add, op1=ALU.subtract,
             )
-        for a in range(2):
+        for i in (1, 0):
             nc.vector.tensor_tensor(
-                out=part_turns[:, a], in0=turns[:, a], in1=whole_turns[:, a], op=ALU.subtract
+                out=part_turns[:, :, i], in0=turns[:, :, i], in1=whole_turns[:, :, i],
+                op=ALU.subtract,
             )
-        table = consts.tile([P, 2, len(phases) + 1, HALF], F32)
+        table = consts.tile([P, 2, 3, HALF], F32)
         nc.scalar.activation(
             out=table[:, :, 1:3, :], in_=part_turns[:], func=ACT.Sin, scale=2.0 * math.pi
         )
@@ -150,7 +144,7 @@ def tile_mla_pb_kernel(tc, hidden_states, w_kv_a, kv_a_ln_w, w_kv_b, out_0, out_
 
         square_sum = consts.tile([P, TOKEN_TILES], F32)
         inv_rms = consts.tile([P, TOKEN_TILES], F32)
-        nc.scalar.activation(out=inv_rms[:, 0:1], in_=inv_freq[:, 0:1], func=ACT.Abs_reciprocal_sqrt)
+        nc.scalar.activation(out=inv_rms[:, 0:1], in_=ones[:, 0:1], func=ACT.Abs_reciprocal_sqrt)
 
         x_codes = resident.tile([P, TOKEN_TILES, PASSES_A * P], U32, align_bytes=64)
         x_scales = resident.tile([P, TOKEN_TILES, PASSES_A * P], U8, align_bytes=64)
@@ -171,17 +165,20 @@ def tile_mla_pb_kernel(tc, hidden_states, w_kv_a, kv_a_ln_w, w_kv_b, out_0, out_
                         )
 
         def regroup_hidden(tt, copies):
-            grouped_x[tt] = stage.tile(
-                [P, PASSES_A * P * PACK], BF16, align_bytes=64, name="grouped_x", tag="grouped_x"
-            )
+            if tt not in grouped_x:
+                grouped_x[tt] = stage.tile(
+                    [P, PASSES_A * P * PACK], BF16, align_bytes=64, name="grouped_x",
+                    tag="grouped_x", bufs=3,
+                )
             grouped_words = grouped_x[tt][:].bitcast(F32).rearrange(
                 "p (g k u) -> p g k u", g=PASSES_A, u=2
             )
             for half, copy in enumerate(copies):
-                copy(
-                    out=grouped_words[:, 2 * half : 2 * half + 2, :, :],
-                    in_=flipped_x[tt, half][:].rearrange("p g u k -> p g k u"),
-                )
+                if copy is not None:
+                    copy(
+                        out=grouped_words[:, 2 * half : 2 * half + 2, :, :],
+                        in_=flipped_x[tt, half][:].rearrange("p g u k -> p g k u"),
+                    )
 
         def quantise_hidden(tt):
             nc.vector.quantize_mx(
@@ -311,7 +308,8 @@ def tile_mla_pb_kernel(tc, hidden_states, w_kv_a, kv_a_ln_w, w_kv_b, out_0, out_
             k_pieces[tt, i] = resident.tile(
                 [P, PIECE_HEADS, NOPE + ROPE], F32, name="k_piece%d_%d" % (tt, i)
             )
-            nc.vector.tensor_copy(
+            copy = nc.scalar.copy if i == 0 else nc.vector.tensor_copy
+            copy(
                 out=k_pieces[tt, i][:, :, NOPE:],
                 in_=k_pe[tt][:].rearrange("p h c -> p (h c)").unsqueeze(1).to_broadcast(
                     [P, PIECE_HEADS, ROPE]
@@ -371,39 +369,34 @@ def tile_mla_pb_kernel(tc, hidden_states, w_kv_a, kv_a_ln_w, w_kv_b, out_0, out_
             copy(out=v_piece[:], in_=by_head(j, tt, KIND_V))
             nc.sync.dma_start(out=v_out[tokens, heads, :], in_=v_piece[:])
 
-        def keep_warm(count):
-            for i in range(count):
-                unread = psum.tile([P, BANK], F32, name="unread", tag="kv_n_or_gain", bufs=1)
-                nc.tensor.matmul(out=unread[:], lhsT=ones[:, 0:P], rhs=ones[:], start=True, stop=True)
-
-        keep_warm(4)
+        for i in range(3):
+            unread = psum.tile([P, BANK], F32, name="unread", tag="kv_n_or_gain", bufs=1)
+            nc.tensor.matmul(out=unread[:], lhsT=ones[:, 0:P], rhs=ones[:], start=True, stop=True)
         flip_hidden(0)
-        keep_warm(6)
         regroup_hidden(0, (nc.vector.tensor_copy, nc.vector.tensor_copy))
         regroup_a(0)
         quantise_hidden(0)
+        gain_ps = psum.tile([P, LATENT], F32, name="gain_ps", tag="kv_n_or_gain", bufs=1)
         for g in range(PASSES_A):
             if g + 1 < PASSES_A:
                 regroup_a(g + 1)
             quantise_a(g)
             latent_pass(0, g)
             if g == 0:
-                keep_warm(2)
-            if g == 1:
-                flip_hidden(1)
-            if g == 2:
-                keep_warm(1)
-        gain_ps = psum.tile([P, LATENT], F32, name="gain_ps", tag="kv_n_or_gain", bufs=1)
-        nc.tensor.matmul(out=gain_ps[:], lhsT=ones[:, 0:P], rhs=gain_row[:], start=True, stop=True)
+                nc.tensor.matmul(
+                    out=gain_ps[:], lhsT=ones[:, 0:P], rhs=gain_row[:], start=True, stop=True
+                )
+            elif g < PASSES_A - 1:
+                flip_hidden(g)
         regroup_hidden(1, (nc.scalar.copy, nc.scalar.copy))
-        rope_passes(0)
-        flip_hidden(2)
-        sum_squares(0)
-        nc.scalar.copy(out=gain[:], in_=gain_ps[:])
-        invert_rms(0)
         quantise_hidden(1)
-        rotate(0)
+        nc.scalar.copy(out=gain[:], in_=gain_ps[:])
+        sum_squares(0)
+        rope_passes(0)
+        invert_rms(0)
+        regroup_hidden(2, (nc.scalar.copy, nc.scalar.copy))
         normalise(0)
+        rotate(0)
         add_k_pe(0)
 
         def is_tile(tt):
@@ -411,14 +404,13 @@ def tile_mla_pb_kernel(tc, hidden_states, w_kv_a, kv_a_ln_w, w_kv_b, out_0, out_
 
         for step in range(TOKEN_TILES + 2):
             if is_tile(step + 2):
-                regroup_hidden(step + 2, (nc.scalar.copy, nc.scalar.copy))
                 quantise_hidden(step + 2)
-            if step < KINDS:
-                regroup_b(0, step)
             if is_tile(step + 1):
                 for g in range(PASSES_A):
                     latent_pass(step + 1, g)
                 sum_squares(step + 1)
+            if step < KINDS:
+                regroup_b(0, step)
             if is_tile(step - 1):
                 multiply_b(0, step - 1, KIND_K_NOPE)
                 store_keys(0, step - 1)
@@ -432,6 +424,7 @@ def tile_mla_pb_kernel(tc, hidden_states, w_kv_a, kv_a_ln_w, w_kv_b, out_0, out_
                 rope_passes(step + 1)
             if is_tile(step + 3):
                 flip_hidden(step + 3)
+                regroup_hidden(step + 3, (nc.scalar.copy, nc.scalar.copy))
             if step < KINDS:
                 quantise_b(0, step)
             if is_tile(step):

@@ -355,9 +355,23 @@ def tile_mla_pb_kernel(tc, hidden_states, w_kv_a, kv_a_ln_w, w_kv_b, out_0, out_
         def by_head(j, tt, kind):
             return kv_ps[j, tt, kind][:].rearrange("p (h c) -> p h c", h=PIECE_HEADS)
 
+        def store_k_pe(tt):
+            tokens = slice(tt * P, (tt + 1) * P)
+            nc.sync.dma_start(
+                out=k_out[tokens, :, NOPE:],
+                in_=k_pe[tt][:].rearrange("p h c -> p (h c)").unsqueeze(1).to_broadcast(
+                    [P, HEADS, ROPE]
+                ),
+            )
+
         def store_keys(j, tt):
             tokens = slice(tt * P, (tt + 1) * P)
             heads = slice(j * PIECE_HEADS, (j + 1) * PIECE_HEADS)
+            if tt == 0:
+                piece = pieces.tile([P, PIECE_HEADS, NOPE], F32, name="nope_piece", tag="nope_piece", bufs=PIECES)
+                nc.scalar.copy(out=piece[:], in_=by_head(j, tt, KIND_K_NOPE))
+                nc.sync.dma_start(out=k_out[tokens, heads, :NOPE], in_=piece[:])
+                return
             piece = k_pieces[tt, j % KEY_TILES]
             nc.scalar.copy(out=piece[:, :, :NOPE], in_=by_head(j, tt, KIND_K_NOPE))
             nc.sync.dma_start(out=k_out[tokens, heads, :], in_=piece[:])
@@ -398,6 +412,7 @@ def tile_mla_pb_kernel(tc, hidden_states, w_kv_a, kv_a_ln_w, w_kv_b, out_0, out_
         normalise(0)
         rotate(0)
         add_k_pe(0)
+        store_k_pe(0)
 
         def is_tile(tt):
             return 0 <= tt < TOKEN_TILES
@@ -427,7 +442,7 @@ def tile_mla_pb_kernel(tc, hidden_states, w_kv_a, kv_a_ln_w, w_kv_b, out_0, out_
                 regroup_hidden(step + 3, (nc.scalar.copy, nc.scalar.copy))
             if step < KINDS:
                 quantise_b(0, step)
-            if is_tile(step):
+            if is_tile(step) and step > 0:
                 spread_k_pe(step, 0)
             if is_tile(step + 1):
                 rotate(step + 1)
@@ -448,7 +463,7 @@ def tile_mla_pb_kernel(tc, hidden_states, w_kv_a, kv_a_ln_w, w_kv_b, out_0, out_
                         regroup_b(j + 1, tt // 2)
                     else:
                         quantise_b(j + 1, tt // 2)
-                if j == 1:
+                if j == 1 and tt > 0:
                     spread_k_pe(tt, 1)
                 for kind in range(KINDS):
                     multiply_b(j, tt, kind)

@@ -44,8 +44,8 @@ PIECES = HEADS // PIECE_HEADS
 KEY_TILES = 2
 
 RUN = 4
-B_SPLIT = (96, 96, 128, 128)
-A_SPLIT = 304
+B_SPLIT = (96, 80, 128, 128)
+A_SPLIT = 256
 
 ROUND_MAGIC = 1.5 * 2.0**23
 
@@ -83,10 +83,12 @@ def tile_mla_pb_kernel(tc, hidden_states, w_kv_a, kv_a_ln_w, w_kv_b, out_0, out_
             rows = w_kv_a[g * K_PASS : (g + 1) * K_PASS, :]
             nc.sync.dma_start(out=raw_a[g][:], in_=rows.rearrange("(p t) c -> p t c", t=PACK))
 
-        def load_b(j):
-            raw_b[j] = resident.tile([P, PACK, PIECE_COLS], BF16, name="raw_b%d" % j)
-            cols = w_kv_b[:, j * PIECE_COLS : (j + 1) * PIECE_COLS]
-            nc.sync.dma_start(out=raw_b[j][:], in_=cols.rearrange("(p t) n -> p t n", t=PACK))
+        def load_b(first, last):
+            raw = resident.tile([P, PACK, (last - first) * PIECE_COLS], BF16, name="raw_b%d" % first)
+            cols = w_kv_b[:, first * PIECE_COLS : last * PIECE_COLS]
+            nc.sync.dma_start(out=raw[:], in_=cols.rearrange("(p t) n -> p t n", t=PACK))
+            for j in range(first, last):
+                raw_b[j] = raw[:, :, (j - first) * PIECE_COLS : (j - first + 1) * PIECE_COLS]
 
         position = consts.tile([P, 2], I32)
         nc.gpsimd.iota(position[:], pattern=[[P, 2]], base=0, channel_multiplier=1)
@@ -101,8 +103,8 @@ def tile_mla_pb_kernel(tc, hidden_states, w_kv_a, kv_a_ln_w, w_kv_b, out_0, out_
         load_gain()
         for tt in range(1, TOKEN_TILES):
             load_x(tt)
-        for j in range(PIECES):
-            load_b(j)
+        load_b(0, 1)
+        load_b(1, PIECES)
 
         warm = consts.tile([P, 1], F32)
         nc.vector.memset(warm[:], 0.0)
@@ -185,20 +187,23 @@ def tile_mla_pb_kernel(tc, hidden_states, w_kv_a, kv_a_ln_w, w_kv_b, out_0, out_
                 out=x_codes[:, tt, :].bitcast(FP8X4), scales=x_scales[:, tt, :], in_=grouped_x[tt][:]
             )
 
-        a_codes = resident.tile([P, PASSES_A, FUSED], U32, align_bytes=64)
-        a_scales = resident.tile([P, PASSES_A, FUSED], U8, align_bytes=64)
+        a_codes = resident.tile([P, PASSES_A, LATENT], U32, align_bytes=64)
+        a_scales = resident.tile([P, PASSES_A, LATENT], U8, align_bytes=64)
+        rope_codes = resident.tile([P, PASSES_A, ROPE], U32, align_bytes=64)
+        rope_scales = resident.tile([P, PASSES_A, ROPE], U8, align_bytes=64)
+        grouped_rope = resident.tile([P, PASSES_A, ROPE, PACK], BF16, align_bytes=64)
         grouped_a = {}
         latent_ps = {}
         rope_ps = {}
 
         def regroup_a(g):
             grouped_a[g] = stage.tile(
-                [P, FUSED, PACK], BF16, align_bytes=64, name="grouped_a", tag="grouped_a",
+                [P, LATENT, PACK], BF16, align_bytes=64, name="grouped_a", tag="grouped_a",
                 bufs=PASSES_A,
             )
             for copy, cols in (
                 (nc.vector.tensor_copy, slice(0, A_SPLIT)),
-                (nc.scalar.copy, slice(A_SPLIT, FUSED)),
+                (nc.scalar.copy, slice(A_SPLIT, LATENT)),
             ):
                 copy(
                     out=grouped_a[g][:, cols, :].rearrange("p (c i) t -> p c t i", i=RUN),
@@ -206,21 +211,33 @@ def tile_mla_pb_kernel(tc, hidden_states, w_kv_a, kv_a_ln_w, w_kv_b, out_0, out_
                 )
 
         def quantise_a(g):
-            for cols in (slice(0, LATENT), slice(LATENT, FUSED)):
-                nc.vector.quantize_mx(
-                    out=a_codes[:, g, cols].bitcast(FP8X4),
-                    scales=a_scales[:, g, cols],
-                    in_=grouped_a[g][:, cols, :].rearrange("p c t -> p (c t)"),
-                )
+            nc.vector.quantize_mx(
+                out=a_codes[:, g, :].bitcast(FP8X4),
+                scales=a_scales[:, g, :],
+                in_=grouped_a[g][:].rearrange("p c t -> p (c t)"),
+            )
 
-        def multiply_a(acc, tt, g, cols):
+        def regroup_rope(g, copy):
+            copy(
+                out=grouped_rope[:, g].rearrange("p (c i) t -> p c t i", i=RUN),
+                in_=raw_a[g][:, :, LATENT:].rearrange("p t (c i) -> p c t i", i=RUN),
+            )
+
+        def quantise_rope():
+            nc.vector.quantize_mx(
+                out=rope_codes[:].rearrange("p g c -> p (g c)").bitcast(FP8X4),
+                scales=rope_scales[:].rearrange("p g c -> p (g c)"),
+                in_=grouped_rope[:].rearrange("p g c t -> p (g c t)"),
+            )
+
+        def multiply_a(acc, tt, g, codes, scales):
             of_pass = slice(g * P, (g + 1) * P)
             nc.tensor.matmul_mx(
                 out=acc[:],
                 lhsT=x_codes[:, tt, of_pass].bitcast(FP8X4),
                 lhsT_scale=x_scales[:, tt, of_pass],
-                rhs=a_codes[:, g, cols].bitcast(FP8X4),
-                rhs_scale=a_scales[:, g, cols],
+                rhs=codes[:, g, :].bitcast(FP8X4),
+                rhs_scale=scales[:, g, :],
                 start=(g == 0),
                 stop=(g == PASSES_A - 1),
             )
@@ -228,12 +245,12 @@ def tile_mla_pb_kernel(tc, hidden_states, w_kv_a, kv_a_ln_w, w_kv_b, out_0, out_
         def latent_pass(tt, g):
             if g == 0:
                 latent_ps[tt] = psum.tile([P, LATENT], F32, name="latent_ps", tag="latent")
-            multiply_a(latent_ps[tt], tt, g, slice(0, LATENT))
+            multiply_a(latent_ps[tt], tt, g, a_codes, a_scales)
 
         def rope_passes(tt):
             rope_ps[tt] = psum.tile([P, ROPE], F32, name="rope_ps", tag="rope", bufs=1)
             for g in range(PASSES_A):
-                multiply_a(rope_ps[tt], tt, g, slice(LATENT, FUSED))
+                multiply_a(rope_ps[tt], tt, g, rope_codes, rope_scales)
 
         n_codes = resident.tile([P, TOKEN_TILES, P], U32, align_bytes=64)
         n_scales = resident.tile([P, TOKEN_TILES, P], U8, align_bytes=64)
@@ -308,7 +325,7 @@ def tile_mla_pb_kernel(tc, hidden_states, w_kv_a, kv_a_ln_w, w_kv_b, out_0, out_
             k_pieces[tt, i] = resident.tile(
                 [P, PIECE_HEADS, NOPE + ROPE], F32, name="k_piece%d_%d" % (tt, i)
             )
-            copy = nc.scalar.copy if i == 0 else nc.vector.tensor_copy
+            copy = nc.vector.tensor_copy
             copy(
                 out=k_pieces[tt, i][:, :, NOPE:],
                 in_=k_pe[tt][:].rearrange("p h c -> p (h c)").unsqueeze(1).to_broadcast(
@@ -320,7 +337,7 @@ def tile_mla_pb_kernel(tc, hidden_states, w_kv_a, kv_a_ln_w, w_kv_b, out_0, out_
             grouped_b[j, kind] = stage.tile(
                 [P, BANK, PACK], BF16, align_bytes=64, name="grouped_b", tag="grouped_b"
             )
-            by_kind = raw_b[j][:].rearrange(
+            by_kind = raw_b[j].rearrange(
                 "p t (h s c i) -> p s h c t i", h=PIECE_HEADS, s=KINDS, i=RUN
             )
             vector_cols = B_SPLIT[j]
@@ -400,19 +417,19 @@ def tile_mla_pb_kernel(tc, hidden_states, w_kv_a, kv_a_ln_w, w_kv_b, out_0, out_
                 nc.tensor.matmul(
                     out=gain_ps[:], lhsT=ones[:, 0:P], rhs=gain_row[:], start=True, stop=True
                 )
-            elif g < PASSES_A - 1:
-                flip_hidden(g)
+            elif g == 1:
+                flip_hidden(1)
+        flip_hidden(2)
+        nc.scalar.copy(out=gain[:], in_=gain_ps[:])
+        for g in range(PASSES_A):
+            regroup_rope(g, nc.vector.tensor_copy)
         regroup_hidden(1, (nc.scalar.copy, nc.scalar.copy))
         quantise_hidden(1)
-        nc.scalar.copy(out=gain[:], in_=gain_ps[:])
         sum_squares(0)
-        rope_passes(0)
         invert_rms(0)
         regroup_hidden(2, (nc.scalar.copy, nc.scalar.copy))
         normalise(0)
-        rotate(0)
-        add_k_pe(0)
-        store_k_pe(0)
+        quantise_rope()
 
         def is_tile(tt):
             return 0 <= tt < TOKEN_TILES
@@ -432,21 +449,23 @@ def tile_mla_pb_kernel(tc, hidden_states, w_kv_a, kv_a_ln_w, w_kv_b, out_0, out_
             if is_tile(step):
                 flip_kv_n(step)
                 regroup_kv_n(step)
+                rope_passes(step)
                 quantise_kv_n(step)
             if is_tile(step + 1):
                 invert_rms(step + 1)
                 normalise(step + 1)
-                rope_passes(step + 1)
             if is_tile(step + 3):
                 flip_hidden(step + 3)
                 regroup_hidden(step + 3, (nc.scalar.copy, nc.scalar.copy))
             if step < KINDS:
                 quantise_b(0, step)
-            if is_tile(step) and step > 0:
+            if is_tile(step):
+                rotate(step)
+                add_k_pe(step)
+            if step == 0:
+                store_k_pe(0)
+            elif is_tile(step):
                 spread_k_pe(step, 0)
-            if is_tile(step + 1):
-                rotate(step + 1)
-                add_k_pe(step + 1)
             if step >= TOKEN_TILES - 1:
                 if step - TOKEN_TILES + 1 < KINDS:
                     regroup_b(1, step - TOKEN_TILES + 1)
@@ -468,4 +487,5 @@ def tile_mla_pb_kernel(tc, hidden_states, w_kv_a, kv_a_ln_w, w_kv_b, out_0, out_
                 for kind in range(KINDS):
                     multiply_b(j, tt, kind)
                 store_keys(j, tt)
-                store_values(j, tt, nc.vector.tensor_copy if tt % 2 == 1 else nc.scalar.copy)
+                by_vector = j == PIECES - 1 and tt % 2 == 1
+                store_values(j, tt, nc.vector.tensor_copy if by_vector else nc.scalar.copy)

@@ -264,6 +264,7 @@ def tile_mla_pb_kernel(tc, hidden_states, w_kv_a, kv_a_ln_w, w_kv_b, out_0, out_
         rotated = {}
         k_pe = {}
         k_pieces = {}
+        v_tiles = {}
         kv_ps = {}
 
         def sum_squares(tt):
@@ -325,8 +326,7 @@ def tile_mla_pb_kernel(tc, hidden_states, w_kv_a, kv_a_ln_w, w_kv_b, out_0, out_
             k_pieces[tt, i] = resident.tile(
                 [P, PIECE_HEADS, NOPE + ROPE], F32, name="k_piece%d_%d" % (tt, i)
             )
-            copy = nc.vector.tensor_copy
-            copy(
+            nc.vector.tensor_copy(
                 out=k_pieces[tt, i][:, :, NOPE:],
                 in_=k_pe[tt][:].rearrange("p h c -> p (h c)").unsqueeze(1).to_broadcast(
                     [P, PIECE_HEADS, ROPE]
@@ -395,10 +395,19 @@ def tile_mla_pb_kernel(tc, hidden_states, w_kv_a, kv_a_ln_w, w_kv_b, out_0, out_
 
         def store_values(j, tt, copy):
             tokens = slice(tt * P, (tt + 1) * P)
-            heads = slice(j * PIECE_HEADS, (j + 1) * PIECE_HEADS)
-            v_piece = pieces.tile([P, PIECE_HEADS, V_DIM], F32, name="v_piece", tag="v_piece")
-            copy(out=v_piece[:], in_=by_head(j, tt, KIND_V))
-            nc.sync.dma_start(out=v_out[tokens, heads, :], in_=v_piece[:])
+            joined = j in (2, 3)
+            if not joined or j == 2:
+                v_tiles[tt] = pieces.tile([P, 2, PIECE_HEADS, V_DIM], F32, name="v_tile", tag="v_tile")
+            half = j - 2 if joined else 0
+            copy(out=v_tiles[tt][:, half], in_=by_head(j, tt, KIND_V))
+            if not joined:
+                heads = slice(j * PIECE_HEADS, (j + 1) * PIECE_HEADS)
+                nc.sync.dma_start(out=v_out[tokens, heads, :], in_=v_tiles[tt][:, 0])
+            elif half == 1:
+                heads = slice((j - 1) * PIECE_HEADS, (j + 1) * PIECE_HEADS)
+                nc.sync.dma_start(
+                    out=v_out[tokens, heads, :], in_=v_tiles[tt][:].rearrange("p a h c -> p (a h) c")
+                )
 
         for i in range(3):
             unread = psum.tile([P, BANK], F32, name="unread", tag="kv_n_or_gain", bufs=1)

import math
from contextlib import ExitStack

import concourse.mybir as mybir
from concourse.masks import make_identity

F32 = mybir.dt.float32
I32 = mybir.dt.int32
BF16 = mybir.dt.bfloat16
U32 = mybir.dt.uint32
U8 = mybir.dt.uint8
FP8X4 = mybir.dt.float8_e4m3fn_x4
ALU = mybir.AluOpType
ACT = mybir.ActivationFunctionType

P = 128
PACK = 4
K_PASS = P * PACK
BANK = 512

TOKENS = 512
TOKEN_TILES = TOKENS // P
D_MODEL = 2048
PASSES_A = D_MODEL // K_PASS
LATENT = 512
ROPE = 128
HALF = ROPE // 2
HALF_LOG2 = 6
assert 2**HALF_LOG2 == HALF
FUSED = LATENT + ROPE
HEADS = 16
NOPE = 128
V_DIM = 128
KINDS = 2
KIND_K_NOPE = 0
KIND_V = 1
ROPE_BASE = 10000.0
EPS = 1e-6

PIECE_HEADS = BANK // NOPE
PIECE_COLS = PIECE_HEADS * (NOPE + V_DIM)
PIECES = HEADS // PIECE_HEADS

KEY_TILES = 2

RUN = 4
B_SPLIT = (96, 80, 128, 128)
A_SPLIT = 256

ROUND_MAGIC = 1.5 * 2.0**23

FLOPS = 2 * TOKENS * D_MODEL * FUSED + 2 * TOKENS * LATENT * HEADS * (NOPE + V_DIM)


def tile_mla_pb_kernel(tc, hidden_states, w_kv_a, kv_a_ln_w, w_kv_b, out_0, out_1):
    nc = tc.nc
    hidden = hidden_states.flatten_outer_dims()
    k_out = out_0.rearrange("b s h c -> (b s) h c")
    v_out = out_1.rearrange("b s h c -> (b s) h c")

    with ExitStack() as ctx:
        ctx.enter_context(tc.manual_schedule())
        consts = ctx.enter_context(tc.tile_pool(name="consts", bufs=1))
        resident = ctx.enter_context(tc.tile_pool(name="resident", bufs=1))
        stage = ctx.enter_context(tc.tile_pool(name="stage", bufs=2))
        pieces = ctx.enter_context(tc.tile_pool(name="pieces", bufs=8))
        psum = ctx.enter_context(tc.psum_pool(name="psum", bufs=2))

        x_rows = {}
        raw_a = {}
        raw_b = {}
        gain_row = consts.tile([P, LATENT], BF16)

        def load_x(tt):
            x_rows[tt] = resident.tile([P, D_MODEL], BF16, name="x_rows%d" % tt)
            nc.sync.dma_start(out=x_rows[tt][:], in_=hidden[tt * P : (tt + 1) * P, :])

        def load_gain():
            nc.sync.dma_start(out=gain_row[0:1, :], in_=kv_a_ln_w.unsqueeze(0))

        def load_a(g):
            raw_a[g] = resident.tile([P, PACK, FUSED], BF16, name="raw_a%d" % g)
            rows = w_kv_a[g * K_PASS : (g + 1) * K_PASS, :]
            nc.sync.dma_start(out=raw_a[g][:], in_=rows.rearrange("(p t) c -> p t c", t=PACK))

        def load_b(first, last):
            raw = resident.tile([P, PACK, (last - first) * PIECE_COLS], BF16, name="raw_b%d" % first)
            cols = w_kv_b[:, first * PIECE_COLS : last * PIECE_COLS]
            nc.sync.dma_start(out=raw[:], in_=cols.rearrange("(p t) n -> p t n", t=PACK))
            for j in range(first, last):
                raw_b[j] = raw[:, :, (j - first) * PIECE_COLS : (j - first + 1) * PIECE_COLS]

        position = consts.tile([P, 2], I32)
        nc.gpsimd.iota(position[:], pattern=[[P, 2]], base=0, channel_multiplier=1)
        ident_f32 = consts.tile([P, P], F32)
        make_identity(nc, ident_f32[:])
        nc.gpsimd.memset(gain_row[:], 0.0)
        ones = consts.tile([P, BANK], BF16)
        nc.vector.memset(ones[:], 1.0)
        load_x(0)
        for g in range(PASSES_A):
            load_a(g)
        load_gain()
        for tt in range(1, TOKEN_TILES):
            load_x(tt)
        load_b(0, 1)
        load_b(1, PIECES)

        warm = consts.tile([P, 1], F32)
        nc.vector.memset(warm[:], 0.0)
        warm_out = consts.tile([P, 1], F32)
        nc.scalar.activation(out=warm_out[:], in_=warm[:], func=ACT.Sin)
        turns = consts.tile([P, 2, 2, HALF], F32)
        whole_turns = consts.tile([P, 2, 2, HALF], F32)
        part_turns = consts.tile([P, 2, 2, HALF], F32)
        nc.vector.tensor_scalar(
            out=turns[:, :, 1, 0:1], in0=position[:].unsqueeze(2), scalar1=1.0 / (2.0 * math.pi),
            scalar2=None, op0=ALU.mult,
        )
        for width in (1, 4, 16):
            for first in range(width, 4 * width, width):
                nc.vector.tensor_scalar(
                    out=turns[:, :, 1, first : first + width], in0=turns[:, :, 1, 0:width],
                    scalar1=ROPE_BASE ** (-first / HALF), scalar2=None, op0=ALU.mult,
                )
        nc.vector.tensor_scalar(
            out=turns[:, :, 0, :], in0=turns[:, :, 1, :], scalar1=0.25, scalar2=None, op0=ALU.add,
        )
        for i in (1, 0):
            nc.vector.tensor_scalar(
                out=whole_turns[:, :, i], in0=turns[:, :, i], scalar1=ROUND_MAGIC,
                scalar2=ROUND_MAGIC, op0=ALU.add, op1=ALU.subtract,
            )
        for i in (1, 0):
            nc.vector.tensor_tensor(
                out=part_turns[:, :, i], in0=turns[:, :, i], in1=whole_turns[:, :, i],
                op=ALU.subtract,
            )
        table = consts.tile([P, 2, 3, HALF], F32)
        nc.scalar.activation(
            out=table[:, :, 1:3, :], in_=part_turns[:], func=ACT.Sin, scale=2.0 * math.pi
        )
        nc.scalar.activation(
            out=table[:, :, 0, :], in_=part_turns[:, :, 1, :], func=ACT.Sin, scale=-2.0 * math.pi
        )

        square_sum = consts.tile([P, TOKEN_TILES], F32)
        inv_rms = consts.tile([P, TOKEN_TILES], F32)
        nc.scalar.activation(out=inv_rms[:, 0:1], in_=ones[:, 0:1], func=ACT.Abs_reciprocal_sqrt)

        x_codes = resident.tile([P, TOKEN_TILES, PASSES_A * P], U32, align_bytes=64)
        x_scales = resident.tile([P, TOKEN_TILES, PASSES_A * P], U8, align_bytes=64)
        flipped_x = {}
        grouped_x = {}

        def flip_hidden(tt):
            words = x_rows[tt][:].bitcast(F32)
            for half in range(2):
                flipped_x[tt, half] = psum.tile([P, 2, 2, P], F32, name="flipped_x", tag="work", bufs=4)
                for gg in range(2):
                    first = (2 * half + gg) * (K_PASS // 2)
                    for u in range(2):
                        nc.tensor.transpose(
                            flipped_x[tt, half][:, gg, u, :],
                            words[:, first + u : first + K_PASS // 2 : 2],
                            ident_f32[:],
                        )

        def regroup_hidden(tt, copies):
            if tt not in grouped_x:
                grouped_x[tt] = stage.tile(
                    [P, PASSES_A * P * PACK], BF16, align_bytes=64, name="grouped_x",
                    tag="grouped_x", bufs=3,
                )
            grouped_words = grouped_x[tt][:].bitcast(F32).rearrange(
                "p (g k u) -> p g k u", g=PASSES_A, u=2
            )
            for half, copy in enumerate(copies):
                if copy is not None:
                    copy(
                        out=grouped_words[:, 2 * half : 2 * half + 2, :, :],
                        in_=flipped_x[tt, half][:].rearrange("p g u k -> p g k u"),
                    )

        def quantise_hidden(tt):
            nc.vector.quantize_mx(
                out=x_codes[:, tt, :].bitcast(FP8X4), scales=x_scales[:, tt, :], in_=grouped_x[tt][:]
            )

        a_codes = resident.tile([P, PASSES_A, LATENT], U32, align_bytes=64)
        a_scales = resident.tile([P, PASSES_A, LATENT], U8, align_bytes=64)
        rope_codes = resident.tile([P, PASSES_A, ROPE], U32, align_bytes=64)
        rope_scales = resident.tile([P, PASSES_A, ROPE], U8, align_bytes=64)
        grouped_rope = resident.tile([P, PASSES_A, ROPE, PACK], BF16, align_bytes=64)
        grouped_a = {}
        latent_ps = {}
        rope_ps = {}

        def regroup_a(g):
            grouped_a[g] = stage.tile(
                [P, LATENT, PACK], BF16, align_bytes=64, name="grouped_a", tag="grouped_a",
                bufs=PASSES_A,
            )
            for copy, cols in (
                (nc.vector.tensor_copy, slice(0, A_SPLIT)),
                (nc.scalar.copy, slice(A_SPLIT, LATENT)),
            ):
                copy(
                    out=grouped_a[g][:, cols, :].rearrange("p (c i) t -> p c t i", i=RUN),
                    in_=raw_a[g][:, :, cols].rearrange("p t (c i) -> p c t i", i=RUN),
                )

        def quantise_a(g):
            nc.vector.quantize_mx(
                out=a_codes[:, g, :].bitcast(FP8X4),
                scales=a_scales[:, g, :],
                in_=grouped_a[g][:].rearrange("p c t -> p (c t)"),
            )

        def regroup_rope(g, copy):
            copy(
                out=grouped_rope[:, g].rearrange("p (c i) t -> p c t i", i=RUN),
                in_=raw_a[g][:, :, LATENT:].rearrange("p t (c i) -> p c t i", i=RUN),
            )

        def quantise_rope():
            nc.vector.quantize_mx(
                out=rope_codes[:].rearrange("p g c -> p (g c)").bitcast(FP8X4),
                scales=rope_scales[:].rearrange("p g c -> p (g c)"),
                in_=grouped_rope[:].rearrange("p g c t -> p (g c t)"),
            )

        def multiply_a(acc, tt, g, codes, scales):
            of_pass = slice(g * P, (g + 1) * P)
            nc.tensor.matmul_mx(
                out=acc[:],
                lhsT=x_codes[:, tt, of_pass].bitcast(FP8X4),
                lhsT_scale=x_scales[:, tt, of_pass],
                rhs=codes[:, g, :].bitcast(FP8X4),
                rhs_scale=scales[:, g, :],
                start=(g == 0),
                stop=(g == PASSES_A - 1),
            )

        def latent_pass(tt, g):
            if g == 0:
                latent_ps[tt] = psum.tile([P, LATENT], F32, name="latent_ps", tag="latent")
            multiply_a(latent_ps[tt], tt, g, a_codes, a_scales)

        def rope_passes(tt):
            rope_ps[tt] = psum.tile([P, ROPE], F32, name="rope_ps", tag="rope", bufs=1)
            for g in range(PASSES_A):
                multiply_a(rope_ps[tt], tt, g, rope_codes, rope_scales)

        n_codes = resident.tile([P, TOKEN_TILES, P], U32, align_bytes=64)
        n_scales = resident.tile([P, TOKEN_TILES, P], U8, align_bytes=64)
        b_codes = resident.tile([P, PIECES, KINDS, BANK], U32, align_bytes=64)
        b_scales = resident.tile([P, PIECES, KINDS, BANK], U8, align_bytes=64)
        gain = consts.tile([P, LATENT], BF16)
        kv_n = {}
        flipped_n = {}
        grouped_n = {}
        grouped_b = {}
        rotated = {}
        k_pe = {}
        k_pieces = {}
        v_tiles = {}
        kv_ps = {}

        def sum_squares(tt):
            squares = stage.tile([P, LATENT], BF16, name="squares", tag="squares")
            nc.scalar.activation(
                out=squares[:], in_=latent_ps[tt][:], func=ACT.Square,
                accum_out=square_sum[:, tt : tt + 1],
            )

        def invert_rms(tt):
            nc.scalar.activation(
                out=inv_rms[:, tt : tt + 1], in_=square_sum[:, tt : tt + 1],
                func=ACT.Abs_reciprocal_sqrt, bias=EPS, scale=1.0 / LATENT,
            )

        def normalise(tt):
            kv_n[tt] = stage.tile([P, LATENT], BF16, name="kv_n", tag="kv_n")
            nc.vector.scalar_tensor_tensor(
                out=kv_n[tt][:], in0=latent_ps[tt][:], scalar=inv_rms[:, tt : tt + 1], in1=gain[:],
                op0=ALU.mult, op1=ALU.mult,
            )

        def flip_kv_n(tt):
            words = kv_n[tt][:].bitcast(F32)
            flipped_n[tt] = psum.tile([P, 2, P], F32, name="flipped_n", tag="kv_n_or_gain", bufs=1)
            for u in range(2):
                nc.tensor.transpose(flipped_n[tt][:, u, :], words[:, u : K_PASS // 2 : 2], ident_f32[:])

        def regroup_kv_n(tt):
            grouped_n[tt] = stage.tile(
                [P, P * PACK], BF16, align_bytes=64, name="grouped_n", tag="grouped_n"
            )
            nc.scalar.copy(
                out=grouped_n[tt][:].bitcast(F32).rearrange("p (k u) -> p k u", u=2),
                in_=flipped_n[tt][:].rearrange("p u k -> p k u"),
            )

        def quantise_kv_n(tt):
            nc.vector.quantize_mx(
                out=n_codes[:, tt, :].bitcast(FP8X4), scales=n_scales[:, tt, :], in_=grouped_n[tt][:]
            )

        def rotate(tt):
            a = tt % 2
            x1 = rope_ps[tt][:, 0:HALF].unsqueeze(1).to_broadcast([P, 2, HALF])
            x2 = rope_ps[tt][:, HALF:ROPE].unsqueeze(1).to_broadcast([P, 2, HALF])
            from_x1 = stage.tile([P, 2, HALF], F32, name="from_x1", tag="from_x1")
            nc.vector.tensor_tensor(out=from_x1[:], in0=x1, in1=table[:, a, 1:3, :], op=ALU.mult)
            from_x2 = stage.tile([P, 2, HALF], F32, name="from_x2", tag="from_x2")
            nc.vector.tensor_tensor(out=from_x2[:], in0=x2, in1=table[:, a, 0:2, :], op=ALU.mult)
            rotated[tt] = (from_x1, from_x2)

        def add_k_pe(tt):
            k_pe[tt] = resident.tile([P, 2, HALF], F32, name="k_pe%d" % tt)
            from_x1, from_x2 = rotated[tt]
            nc.vector.tensor_tensor(out=k_pe[tt][:], in0=from_x1[:], in1=from_x2[:], op=ALU.add)

        def spread_k_pe(tt, i):
            k_pieces[tt, i] = resident.tile(
                [P, PIECE_HEADS, NOPE + ROPE], F32, name="k_piece%d_%d" % (tt, i)
            )
            nc.vector.tensor_copy(
                out=k_pieces[tt, i][:, :, NOPE:],
                in_=k_pe[tt][:].rearrange("p h c -> p (h c)").unsqueeze(1).to_broadcast(
                    [P, PIECE_HEADS, ROPE]
                ),
            )

        def regroup_b(j, kind):
            grouped_b[j, kind] = stage.tile(
                [P, BANK, PACK], BF16, align_bytes=64, name="grouped_b", tag="grouped_b"
            )
            by_kind = raw_b[j].rearrange(
                "p t (h s c i) -> p s h c t i", h=PIECE_HEADS, s=KINDS, i=RUN
            )
            vector_cols = B_SPLIT[j]
            by_run = grouped_b[j, kind][:].rearrange("p (h c i) t -> p h c t i", h=PIECE_HEADS, i=RUN)
            for copy, runs in (
                (nc.vector.tensor_copy, slice(0, vector_cols // RUN)),
                (nc.scalar.copy, slice(vector_cols // RUN, NOPE // RUN)),
            ):
                if runs.start < runs.stop:
                    for_kind = by_kind[:, kind]
                    copy(out=by_run[:, :, runs], in_=for_kind[:, :, runs])

        def quantise_b(j, kind):
            nc.vector.quantize_mx(
                out=b_codes[:, j, kind, :].bitcast(FP8X4),
                scales=b_scales[:, j, kind, :],
                in_=grouped_b[j, kind][:].rearrange("p c t -> p (c t)"),
            )

        def multiply_b(j, tt, kind):
            kv_ps[j, tt, kind] = psum.tile([P, BANK], F32, name="kv_ps", tag="work", bufs=4)
            nc.tensor.matmul_mx(
                out=kv_ps[j, tt, kind][:],
                lhsT=n_codes[:, tt, :].bitcast(FP8X4),
                lhsT_scale=n_scales[:, tt, :],
                rhs=b_codes[:, j, kind, :].bitcast(FP8X4),
                rhs_scale=b_scales[:, j, kind, :],
                start=True,
                stop=True,
            )

        def by_head(j, tt, kind):
            return kv_ps[j, tt, kind][:].rearrange("p (h c) -> p h c", h=PIECE_HEADS)

        def store_k_pe(tt):
            tokens = slice(tt * P, (tt + 1) * P)
            nc.sync.dma_start(
                out=k_out[tokens, :, NOPE:],
                in_=k_pe[tt][:].rearrange("p h c -> p (h c)").unsqueeze(1).to_broadcast(
                    [P, HEADS, ROPE]
                ),
            )

        def store_keys(j, tt):
            tokens = slice(tt * P, (tt + 1) * P)
            heads = slice(j * PIECE_HEADS, (j + 1) * PIECE_HEADS)
            if tt == 0:
                piece = pieces.tile([P, PIECE_HEADS, NOPE], F32, name="nope_piece", tag="nope_piece", bufs=PIECES)
                nc.scalar.copy(out=piece[:], in_=by_head(j, tt, KIND_K_NOPE))
                nc.sync.dma_start(out=k_out[tokens, heads, :NOPE], in_=piece[:])
                return
            piece = k_pieces[tt, j % KEY_TILES]
            nc.scalar.copy(out=piece[:, :, :NOPE], in_=by_head(j, tt, KIND_K_NOPE))
            nc.sync.dma_start(out=k_out[tokens, heads, :], in_=piece[:])

        def store_values(j, tt, copy):
            tokens = slice(tt * P, (tt + 1) * P)
            joined = j in (2, 3)
            if not joined or j == 2:
                v_tiles[tt] = pieces.tile([P, 2, PIECE_HEADS, V_DIM], F32, name="v_tile", tag="v_tile")
            half = j - 2 if joined else 0
            copy(out=v_tiles[tt][:, half], in_=by_head(j, tt, KIND_V))
            if not joined:
                heads = slice(j * PIECE_HEADS, (j + 1) * PIECE_HEADS)
                nc.sync.dma_start(out=v_out[tokens, heads, :], in_=v_tiles[tt][:, 0])
            elif half == 1:
                heads = slice((j - 1) * PIECE_HEADS, (j + 1) * PIECE_HEADS)
                nc.sync.dma_start(
                    out=v_out[tokens, heads, :], in_=v_tiles[tt][:].rearrange("p a h c -> p (a h) c")
                )

        for i in range(3):
            unread = psum.tile([P, BANK], F32, name="unread", tag="kv_n_or_gain", bufs=1)
            nc.tensor.matmul(out=unread[:], lhsT=ones[:, 0:P], rhs=ones[:], start=True, stop=True)
        flip_hidden(0)
        regroup_hidden(0, (nc.vector.tensor_copy, nc.vector.tensor_copy))
        regroup_a(0)
        quantise_hidden(0)
        gain_ps = psum.tile([P, LATENT], F32, name="gain_ps", tag="kv_n_or_gain", bufs=1)
        for g in range(PASSES_A):
            if g + 1 < PASSES_A:
                regroup_a(g + 1)
            quantise_a(g)
            latent_pass(0, g)
            if g == 0:
                nc.tensor.matmul(
                    out=gain_ps[:], lhsT=ones[:, 0:P], rhs=gain_row[:], start=True, stop=True
                )
            elif g == 1:
                flip_hidden(1)
        flip_hidden(2)
        nc.scalar.copy(out=gain[:], in_=gain_ps[:])
        for g in range(PASSES_A):
            regroup_rope(g, nc.vector.tensor_copy)
        regroup_hidden(1, (nc.scalar.copy, nc.scalar.copy))
        quantise_hidden(1)
        sum_squares(0)
        invert_rms(0)
        regroup_hidden(2, (nc.scalar.copy, nc.scalar.copy))
        normalise(0)
        quantise_rope()

        def is_tile(tt):
            return 0 <= tt < TOKEN_TILES

        for step in range(TOKEN_TILES + 2):
            if is_tile(step + 2):
                quantise_hidden(step + 2)
            if is_tile(step + 1):
                for g in range(PASSES_A):
                    latent_pass(step + 1, g)
                sum_squares(step + 1)
            if step < KINDS:
                regroup_b(0, step)
            if is_tile(step - 1):
                multiply_b(0, step - 1, KIND_K_NOPE)
                store_keys(0, step - 1)
            if is_tile(step):
                flip_kv_n(step)
                regroup_kv_n(step)
                rope_passes(step)
                quantise_kv_n(step)
            if is_tile(step + 1):
                invert_rms(step + 1)
                normalise(step + 1)
            if is_tile(step + 3):
                flip_hidden(step + 3)
                regroup_hidden(step + 3, (nc.scalar.copy, nc.scalar.copy))
            if step < KINDS:
                quantise_b(0, step)
            if is_tile(step):
                rotate(step)
                add_k_pe(step)
            if step == 0:
                store_k_pe(0)
            elif is_tile(step):
                spread_k_pe(step, 0)
            if step >= TOKEN_TILES - 1:
                if step - TOKEN_TILES + 1 < KINDS:
                    regroup_b(1, step - TOKEN_TILES + 1)
                if step - TOKEN_TILES >= 0:
                    quantise_b(1, step - TOKEN_TILES)
            if is_tile(step - 2):
                multiply_b(0, step - 2, KIND_V)
                store_values(0, step - 2, nc.scalar.copy)

        for j in range(1, PIECES):
            for tt in range(TOKEN_TILES):
                if j + 1 < PIECES:
                    if tt % 2 == 0:
                        regroup_b(j + 1, tt // 2)
                    else:
                        quantise_b(j + 1, tt // 2)
                if j == 1 and tt > 0:
                    spread_k_pe(tt, 1)
                for kind in range(KINDS):
                    multiply_b(j, tt, kind)
                store_keys(j, tt)
                by_vector = j == PIECES - 1 and tt % 2 == 1
                store_values(j, tt, nc.vector.tensor_copy if by_vector else nc.scalar.copy)
